import numpy as np
import ml_dtypes


def mxq(x, axis, fmt="e4m3"):
    dtype, down = {"e4m3": (ml_dtypes.float8_e4m3fn, 7), "e5m2": (ml_dtypes.float8_e5m2, 14)}[fmt]
    v = np.moveaxis(np.asarray(x, np.float32).astype(ml_dtypes.bfloat16).astype(np.float64), axis, -1)
    blocks = v.reshape(v.shape[:-1] + (-1, 32))
    amax = np.abs(blocks).max(-1, keepdims=True)
    byte = np.maximum(np.where(amax > 0, np.frexp(amax)[1] - 1 + 127, 0) - down, 1)
    scale = np.exp2(byte - 127.0)
    codes = (blocks / scale).astype(np.float32).astype(dtype).astype(np.float64)
    return np.moveaxis((codes * scale).reshape(v.shape), -1, axis)


WIDE = False


def mx_kscale(k):
    if not WIDE:
        return np.ones(k)
    levels = np.array([18, -18])
    if k % 512:
        return np.exp2(np.random.permutation(np.resize(levels, k // 32))).repeat(32)
    a = np.empty((k // 512, 16))
    for p in range(k // 512):
        a[p, :8] = np.random.permutation(np.resize(levels, 8))
        for g in range(8):
            far = levels[np.abs(levels - a[p, g]) >= 10]
            a[p, g + 8] = far[np.random.randint(len(far))]
    return np.exp2(a.ravel()).repeat(32)


BF16 = ml_dtypes.bfloat16


def bf(x):
    return np.asarray(x, np.float32).astype(BF16)


def f64(x):
    return np.asarray(x).astype(np.float64)


B, H, W, C = 512, 2, 2, 1024
G = C // 4
NBR = 3


def gate_softmax(gate_hid, wa2, ba2):
    z = f64(gate_hid) @ f64(wa2) + f64(ba2)
    z = z.reshape(B, C, NBR).transpose(2, 0, 1)
    e = np.exp(z - z.max(0, keepdims=True))
    return e / e.sum(0, keepdims=True)


def setup_inputs():
    s = mx_kscale(B)
    u = mx_kscale(C)
    v = mx_kscale(C)
    v3 = np.repeat(v, NBR)
    h_mix = bf(0.8 * np.random.standard_normal((B, H, W, C)))
    w_mix = bf(0.8 * np.random.standard_normal((B, H, W, C)))
    c_proj = bf(np.random.standard_normal((B, H, W, C)))
    gate_hid0 = bf(0.6 * np.random.standard_normal((B, G)))
    wa2_0 = bf(2.0 * np.random.standard_normal((G, C * NBR)) / np.sqrt(G))
    ba2 = bf(0.6 * np.random.standard_normal(C * NBR))
    wo0 = bf(np.random.standard_normal((C, C)) / np.sqrt(C))
    bo = bf(0.3 * np.random.standard_normal(C))
    g = np.random.standard_normal((B, H, W, C)) * np.exp2(np.random.randint(-6, 1, (B, H, W, 1)))
    g = bf(g / s[:, None, None, None] * u)
    gate = gate_softmax(gate_hid0, wa2_0, ba2)
    return {
        "h_mix": h_mix,
        "w_mix": w_mix,
        "c_proj": c_proj,
        "gate_hid": bf(f64(gate_hid0) * s[:, None]),
        "wa2": bf(f64(wa2_0) / v3),
        "ba2": ba2,
        "wo": bf(f64(wo0) * v[:, None] / u),
        "bo": bo,
        "gate": np.asarray(gate, np.float32),
        "grad_out": g,
    }


def reference(h_mix, w_mix, c_proj, gate_hid, wa2, ba2, wo, bo, gate, grad_out):
    p = f64(gate)
    g2 = f64(grad_out).reshape(B * H * W, C)
    dfused = mxq(g2, 1, "e5m2") @ mxq(f64(wo), 1, "e4m3").T
    dfused = dfused.reshape(B, H * W, C)
    dp = np.stack([(dfused * f64(t).reshape(B, H * W, C)).sum(1) for t in (h_mix, w_mix, c_proj)])
    dz = p * (dp - (p * dp).sum(0, keepdims=True))
    dz = dz.transpose(1, 2, 0).reshape(B, C * NBR)
    dgate_hid = mxq(dz, 1, "e5m2") @ mxq(f64(wa2), 1, "e4m3").T
    dwa2 = mxq(f64(gate_hid), 0, "e4m3").T @ mxq(dz, 0, "e5m2")
    return dgate_hid, dwa2

@@ -1,0 +1,421 @@
+from contextlib import ExitStack
+
+import concourse.mybir as mybir
+from concourse.masks import make_identity
+
+F32 = mybir.dt.float32
+BF16 = mybir.dt.bfloat16
+U32 = mybir.dt.uint32
+U8 = mybir.dt.uint8
+E4M3 = mybir.dt.float8_e4m3fn_x4
+E5M2 = mybir.dt.float8_e5m2_x4
+MULT = mybir.AluOpType.mult
+ADD = mybir.AluOpType.add
+SUB = mybir.AluOpType.subtract
+
+B, POS, C, G, K3 = 512, 4, 1024, 256, 3
+L = C * K3
+P = 128
+NT = 4
+HALF = 512
+LH = HALF * K3
+NU = 8
+
+FLOPS = 2 * B * POS * C * C + 2 * 2 * B * L * G
+BYTES = 2 * (4 * B * POS * C + B * G + G * L + C * C) + 4 * (K3 * B * C + B * G + G * L)
+
+
+def tile_hiremodule_pc_v_kernel(
+    tc, h_mix, w_mix, c_proj, gate_hid, wa2, ba2, wo, bo, gate, grad_out, out_0, out_1
+):
+    nc = tc.nc
+    with ExitStack() as ctx:
+        keep = ctx.enter_context(tc.tile_pool(name="keep", bufs=1))
+        ring = ctx.enter_context(tc.tile_pool(name="ring", bufs=2))
+        psum = ctx.enter_context(tc.psum_pool(name="psum", bufs=2))
+        ctx.enter_context(tc.manual_schedule())
+
+        streams = [x.rearrange("(p t) i j c -> p t (i j) c", t=NT) for x in (h_mix, w_mix, c_proj)]
+        g_view = grad_out.rearrange("(p t) i j c -> p t (i j) c", t=NT)
+        gate_view = gate.rearrange("k (p t) c -> p k t c", t=NT)
+        out0_view = out_0.rearrange("(p t) g -> p t g", t=NT)
+
+        ident = keep.tile([P, P], F32, name="ident")
+        make_identity(nc, ident[:])
+
+        wo_codes = keep.tile([P, 2, 2, HALF], U32, name="wo_codes", align_bytes=64)
+        wo_scales = keep.tile([P, 2, 2, HALF], U8, name="wo_scales", align_bytes=64)
+        wa2_codes = keep.tile([P, 7 * G], U32, name="wa2_codes", align_bytes=64)
+        wa2_scales = keep.tile([P, 7 * G], U8, name="wa2_scales", align_bytes=64)
+        gh_codes = keep.tile([P, G], U32, name="gh_codes", align_bytes=64)
+        gh_scales = keep.tile([P, G], U8, name="gh_scales", align_bytes=64)
+        x1 = [keep.tile([P, LH, 4], BF16, name="x1_%d" % h, align_bytes=64) for h in range(2)]
+        nc.gpsimd.memset(wa2_codes[:, 6 * G : 7 * G], 0)
+        nc.gpsimd.memset(wa2_scales[:, 6 * G : 7 * G], 0)
+
+        def nat_tile(name):
+            return ring.tile([P, 4, C], BF16, name=name, tag="nat", bufs=3)
+
+        wo_nat, g_nat, wa2_nat, st, gate_t = {}, {}, {}, {}, {}
+
+        def load_wo(h):
+            wo_nat[h] = nat_tile("wo_nat%d" % h)
+            v = wo[h * HALF : (h + 1) * HALF, :].rearrange("(c p) o -> p c o", p=P)
+            for c in (0, 2):
+                nc.sync.dma_start(out=wo_nat[h][:, c : c + 2, :], in_=v[:, c : c + 2, :])
+
+        def load_g(t):
+            g_nat[t] = nat_tile("g_nat%d" % t)
+            for c in (0, 2):
+                nc.sync.dma_start(out=g_nat[t][:, c : c + 2, :], in_=g_view[:, t, c : c + 2, :])
+
+        def load_wa2(w):
+            wa2_nat[w] = ring.tile([P, 2, LH], BF16, name="wa2_nat%d" % w, tag="nat", bufs=3)
+            v = wa2.rearrange("(m p) l -> p m l", p=P)
+            nc.sync.dma_start(out=wa2_nat[w][:], in_=v[:, :, w * LH : (w + 1) * LH])
+
+        def load_st(t, pp):
+            for k in range(K3):
+                st[t, k, pp] = ring.tile([P, 2, C], BF16, name="st%d%d%d" % (t, k, pp), tag="st", bufs=10)
+                nc.sync.dma_start(out=st[t, k, pp][:], in_=streams[k][:, t, 2 * pp : 2 * pp + 2, :])
+
+        def load_gate(t, h):
+            gate_t[t, h] = ring.tile([P, K3, HALF], F32, name="gate%d%d" % (t, h), tag="gate", bufs=3)
+            nc.sync.dma_start(out=gate_t[t, h][:], in_=gate_view[:, :, t, h * HALF : (h + 1) * HALF])
+
+        load_wo(0)
+        load_g(0)
+        load_st(0, 0)
+        load_st(0, 1)
+        load_wo(1)
+        load_gate(0, 0)
+        load_g(1)
+        load_wa2(0)
+        load_gate(0, 1)
+        load_wa2(1)
+        load_st(1, 0)
+        load_st(1, 1)
+        load_gate(1, 0)
+        load_g(2)
+        load_gate(1, 1)
+        gh_raw = keep.tile([P, 4, G], BF16, name="gh_raw")
+        nc.sync.dma_start(out=gh_raw[:], in_=gate_hid.rearrange("(p j) w -> p j w", j=4))
+        load_st(2, 0)
+        load_st(2, 1)
+        load_gate(2, 0)
+        load_g(3)
+        load_gate(2, 1)
+        load_st(3, 0)
+        load_st(3, 1)
+        load_gate(3, 0)
+        load_gate(3, 1)
+
+        PS_BUFS = {"tp": 2, "df": 2, "dp": 3, "o0": 1}
+
+        def bank(tag, name):
+            return psum.tile([P, HALF], F32, name=name, tag=tag, bufs=PS_BUFS[tag])
+
+        def copy_out(engine, out, in_):
+            if engine == "S":
+                nc.scalar.copy(out, in_)
+            else:
+                nc.vector.tensor_copy(out, in_)
+
+        def word_transposes(bk, srcs):
+            for n, src in enumerate(srcs):
+                nc.tensor.transpose(bk[:, n * P : (n + 1) * P], src, ident[:])
+
+        def grp_tile(width, name):
+            return ring.tile([P, width], BF16, name=name, tag="grp", bufs=3, align_bytes=64)
+
+        def wo_prep(h, tags, engines):
+            grp = [grp_tile(4 * HALF, "wo_grp%d%d" % (h, g)) for g in range(2)]
+            words = wo_nat[h][:].bitcast(F32)
+            for c in range(4):
+                bk = bank(tags[c % len(tags)], "wo_ps%d%d" % (h, c))
+                word_transposes(bk, [words[:, c, 256 * g + u : 256 * (g + 1) : 2] for g in range(2) for u in range(2)])
+                for g in range(2):
+                    dst = grp[g][:, 4 * P * c : 4 * P * (c + 1)].bitcast(F32).rearrange("p (r u) -> p r u", u=2)
+                    src = bk[:, 256 * g : 256 * (g + 1)].rearrange("p (u r) -> p r u", u=2)
+                    copy_out(engines[c % len(engines)], dst, src)
+            return grp
+
+        def wo_quant(h, grp):
+            for g in range(2):
+                nc.vector.quantize_mx(out=wo_codes[:, h, g, :].bitcast(E4M3), scales=wo_scales[:, h, g, :], in_=grp[g][:])
+
+        g_codes, g_scales, g_grp = {}, {}, {}
+
+        def g_prep(s, tags, engines):
+            t, pair = divmod(s, 2)
+            if pair == 0:
+                g_codes[t] = ring.tile([P, 8 * P], U32, name="g_codes%d" % t, tag="g_codes", bufs=2, align_bytes=64)
+                g_scales[t] = ring.tile([P, 8 * P], U8, name="g_scales%d" % t, tag="g_scales", bufs=2, align_bytes=64)
+            g_grp[s] = grp_tile(2048, "g_grp%d" % s)
+            words = g_nat[t][:].bitcast(F32)
+            for q in range(2):
+                bk = bank(tags[q % len(tags)], "g_ps%d%d" % (s, q))
+                word_transposes(bk, [words[:, 2 * pair + q, 256 * g + u : 256 * (g + 1) : 2] for g in range(2) for u in range(2)])
+                dst = g_grp[s][:, 1024 * q : 1024 * (q + 1)].bitcast(F32).rearrange("p (g r u) -> p g r u", g=2, u=2)
+                src = bk[:].rearrange("p (g u r) -> p g r u", g=2, u=2)
+                copy_out(engines[q % len(engines)], dst, src)
+
+        def g_quant(s):
+            t, pair = divmod(s, 2)
+            sl = slice(512 * pair, 512 * (pair + 1))
+            nc.vector.quantize_mx(out=g_codes[t][:, sl].bitcast(E5M2), scales=g_scales[t][:, sl], in_=g_grp[s][:])
+
+        def wa2_prep(n, tag, engine):
+            w, j = divmod(n, 3)
+            words = wa2_nat[w][:].bitcast(F32)
+            bk = bank(tag, "wa2_ps%d" % n)
+            word_transposes(bk, [words[:, m, 256 * j + u : 256 * (j + 1) : 2] for m in range(2) for u in range(2)])
+            grp = grp_tile(1024, "wa2_grp%d" % n)
+            dst = grp[:].bitcast(F32).rearrange("p (m r u) -> p m r u", m=2, u=2)
+            src = bk[:].rearrange("p (m u r) -> p m r u", m=2, u=2)
+            copy_out(engine, dst, src)
+            return grp
+
+        def wa2_quant(n, grp):
+            sl = slice(G * n, G * (n + 1))
+            nc.vector.quantize_mx(out=wa2_codes[:, sl].bitcast(E4M3), scales=wa2_scales[:, sl], in_=grp[:])
+
+        df_bank, dfc, prod, dp_bank, dpt, qe, mm, z, dzg, dzc, dzs, o0_bank = {}, {}, {}, {}, {}, {}, {}, {}, {}, {}, {}, {}
+        o0_sb = keep.tile([P, NT, G], F32, name="o0_sb")
+
+        def df(i, pos):
+            if i >= NU:
+                return
+            t, h = divmod(i, 2)
+            bk = bank("df", "df%d%d" % (i, pos))
+            df_bank[i, pos] = bk
+            for g in range(2):
+                sl = slice(P * (2 * pos + g), P * (2 * pos + g + 1))
+                nc.tensor.matmul_mx(
+                    out=bk[:],
+                    lhsT=g_codes[t][:, sl].bitcast(E5M2),
+                    lhsT_scale=g_scales[t][:, sl],
+                    rhs=wo_codes[:, h, g, :].bitcast(E4M3),
+                    rhs_scale=wo_scales[:, h, g, :],
+                    start=(g == 0),
+                    stop=(g == 1),
+                )
+
+        def df_copy(i, pos):
+            if i >= NU:
+                return
+            dfc[i] = ring.tile([P, HALF], F32, name="dfc%d" % i, tag="dfc", bufs=2)
+            nc.scalar.copy(dfc[i][:], df_bank[i, pos][:])
+
+        def products(i, pos, engine):
+            t, h = divmod(i, 2)
+            for k in range(K3):
+                pt = ring.tile([P, HALF], F32, name="prod%d%d%d" % (i, pos, k), tag="prod", bufs=16)
+                prod[i, pos, k] = pt
+                s_ap = st[t, k, pos // 2][:, pos % 2, h * HALF : (h + 1) * HALF]
+                if engine == "G":
+                    nc.gpsimd.tensor_tensor(out=pt[:], in0=dfc[i][:], in1=s_ap, op=MULT)
+                else:
+                    nc.vector.tensor_tensor(out=pt[:], in0=df_bank[i, pos][:], in1=s_ap, op=MULT)
+
+        def pacc(i, k):
+            bk = bank("tp", "pacc%d%d" % (i, k))
+            for c in range(4):
+                cs = slice(P * c, P * (c + 1))
+                for pos in range(POS):
+                    nc.tensor.matmul(
+                        bk[:, cs], prod[i, pos, k][:, cs], ident[:], start=(pos == 0), stop=(pos == POS - 1), is_transpose=True
+                    )
+            dpt[i, k] = ring.tile([P, HALF], F32, name="dpt%d%d" % (i, k), tag="dpt", bufs=2)
+            nc.scalar.copy(dpt[i, k][:], bk[:])
+
+        def back(i, k):
+            bk = bank("dp", "dp%d%d" % (i, k))
+            dp_bank[i, k] = bk
+            word_transposes(bk, [dpt[i, k][:, P * c : P * (c + 1)] for c in range(4)])
+
+        def q_step(i):
+            t, h = divmod(i, 2)
+            qe[i] = ring.tile([P, K3, HALF], F32, name="qe%d" % i, tag="qe", bufs=2)
+            for k in range(K3):
+                nc.vector.tensor_tensor(out=qe[i][:, k, :], in0=dp_bank[i, k][:], in1=gate_t[t, h][:, k, :], op=MULT)
+
+        def m_step(i):
+            m0 = ring.tile([P, HALF], F32, name="m0_%d" % i, tag="m", bufs=2)
+            nc.gpsimd.tensor_tensor(out=m0[:], in0=qe[i][:, 0, :], in1=qe[i][:, 1, :], op=ADD)
+            m1 = ring.tile([P, HALF], F32, name="m1_%d" % i, tag="m", bufs=2)
+            mm[i] = m1
+            nc.gpsimd.tensor_tensor(out=m1[:], in0=m0[:], in1=qe[i][:, 2, :], op=ADD)
+
+        def e_step(i):
+            for k in range(K3):
+                nc.vector.tensor_tensor(out=qe[i][:, k, :], in0=dp_bank[i, k][:], in1=mm[i][:], op=SUB)
+
+        def dz_step(i, parts):
+            t, h = divmod(i, 2)
+            if t % 2 == 0:
+                z[t // 2, h] = ring.tile([P, 2, LH], BF16, name="z%d%d" % (t, h), tag="z", bufs=2)
+            zt = z[t // 2, h]
+            for engine, lo, hi in parts:
+                o = zt[:, t % 2, K3 * lo : K3 * hi].rearrange("p (c k) -> p c k", k=K3)
+                a = gate_t[t, h][:, :, lo:hi].rearrange("p k c -> p c k")
+                b = qe[i][:, :, lo:hi].rearrange("p k c -> p c k")
+                eng = nc.gpsimd if engine == "G" else nc.vector
+                eng.tensor_tensor(out=o, in0=a, in1=b, op=MULT)
+
+        def x1_step(i, parts):
+            t, h = divmod(i, 2)
+            if t % 2 == 0:
+                return
+            u = t // 2
+            for engine, lo, hi in parts:
+                copy_out(engine, x1[h][:, lo:hi, 2 * u : 2 * u + 2], z[u, h][:, :, lo:hi].rearrange("p t l -> p l t"))
+
+        def dzt_step(i):
+            t, h = divmod(i, 2)
+            words = z[t // 2, h][:].bitcast(F32)
+            dzg[i] = ring.tile([P, K3 * 512], BF16, name="dzg%d" % i, tag="dzg", bufs=2, align_bytes=64)
+            for j0, nj in ((0, 2), (2, 1)):
+                bk = bank("tp", "dzt%d%d" % (i, j0))
+                word_transposes(
+                    bk,
+                    [words[:, t % 2, 256 * j + u : 256 * (j + 1) : 2] for j in range(j0, j0 + nj) for u in range(2)],
+                )
+                dst = dzg[i][:, 512 * j0 : 512 * (j0 + nj)].bitcast(F32).rearrange("p (j r u) -> p j r u", j=nj, u=2)
+                src = bk[:, 0 : 256 * nj].rearrange("p (j u r) -> p j r u", j=nj, u=2)
+                nc.scalar.copy(dst, src)
+
+        def dz_quant(i):
+            dzc[i] = ring.tile([P, K3 * P], U32, name="dzc%d" % i, tag="dzc", bufs=2, align_bytes=64)
+            dzs[i] = ring.tile([P, K3 * P], U8, name="dzs%d" % i, tag="dzs", bufs=2, align_bytes=64)
+            for lo, hi in ((0, 2), (2, 3)):
+                sl = slice(P * lo, P * hi)
+                nc.vector.quantize_mx(out=dzc[i][:, sl].bitcast(E5M2), scales=dzs[i][:, sl], in_=dzg[i][:, 512 * lo : 512 * hi])
+
+        def out0_step(i):
+            t, h = divmod(i, 2)
+            if h == 0:
+                o0_bank[t] = bank("o0", "o0_%d" % t)
+            for j in range(K3):
+                n = K3 * h + j
+                nc.tensor.matmul_mx(
+                    out=o0_bank[t][:],
+                    lhsT=dzc[i][:, P * j : P * (j + 1)].bitcast(E5M2),
+                    lhsT_scale=dzs[i][:, P * j : P * (j + 1)],
+                    rhs=wa2_codes[:, G * n : G * n + 512].bitcast(E4M3),
+                    rhs_scale=wa2_scales[:, G * n : G * n + 512],
+                    start=(n == 0),
+                    stop=(n == 5),
+                )
+            if h == 1:
+                nc.scalar.copy(o0_sb[:, t, :], o0_bank[t][:, 0:G])
+                nc.sync.dma_start(out=out0_view[:, t, :], in_=o0_sb[:, t, :])
+
+        def out1_quant(h, n):
+            xc = ring.tile([P, 512], U32, name="xc%d%d" % (h, n), tag="xc", bufs=2, align_bytes=64)
+            xs = ring.tile([P, 512], U8, name="xs%d%d" % (h, n), tag="xs", bufs=2, align_bytes=64)
+            nc.vector.quantize_mx(
+                out=xc[:].bitcast(E5M2),
+                scales=xs[:],
+                in_=x1[h][:, 512 * n : 512 * (n + 1), :].rearrange("p l t -> p (l t)"),
+            )
+            return xc, xs
+
+        def out1_mm(h, n, xc, xs, tags, engines):
+            for m in range(2):
+                bk = bank(tags[m], "o1_%d%d%d" % (h, n, m))
+                nc.tensor.matmul_mx(
+                    out=bk[:],
+                    lhsT=gh_codes[:, P * m : P * (m + 1)].bitcast(E4M3),
+                    lhsT_scale=gh_scales[:, P * m : P * (m + 1)],
+                    rhs=xc[:].bitcast(E5M2),
+                    rhs_scale=xs[:],
+                    start=True,
+                    stop=True,
+                )
+                ot = ring.tile([P, 512], F32, name="ot%d%d%d" % (h, n, m), tag="prod", bufs=16)
+                copy_out(engines[m], ot[:], bk[:])
+                l0 = LH * h + 512 * n
+                nc.sync.dma_start(out=out_1[P * m : P * (m + 1), l0 : l0 + 512], in_=ot[:])
+
+        grp0 = wo_prep(0, ["tp", "dp", "df"], ["S", "V"])
+        wo_quant(0, grp0)
+        g_prep(0, ["tp", "dp"], ["S", "V"])
+        g_quant(0)
+        g_prep(1, ["tp", "dp"], ["S", "V"])
+        df(0, 0)
+        df_copy(0, 0)
+        df(0, 1)
+        g_quant(1)
+        df(0, 2)
+        grp1 = wo_prep(1, ["tp", "dp"], ["S"])
+
+        for i in range(NU):
+            products(i, 0, "G")
+            if i > 0:
+                pacc(i - 1, 2)
+                back(i - 1, 1)
+                back(i - 1, 2)
+            products(i, 1, "V")
+            df(i, 3)
+            if i + 2 < NU:
+                g_prep(i + 2, ["tp"], ["S"])
+            if i == 0:
+                wo_quant(1, grp1)
+            products(i, 2, "V")
+            df(i + 1, 0)
+            df_copy(i + 1, 0)
+            if i >= 2:
+                dzt_step(i - 2)
+                dz_quant(i - 2)
+            if i + 2 < NU:
+                g_quant(i + 2)
+            if i < 3:
+                grp = [wa2_prep(2 * i + n, "tp", "S") for n in range(2)]
+                for n in range(2):
+                    wa2_quant(2 * i + n, grp[n])
+            if i >= 1:
+                q_step(i - 1)
+                m_step(i - 1)
+            df(i + 1, 1)
+            if i >= 2:
+                x1_step(i - 2, [("S", 0, LH)])
+            products(i, 3, "V")
+            pacc(i, 0)
+            df(i + 1, 2)
+            if i >= 1:
+                e_step(i - 1)
+                dz_step(i - 1, [("G", 0, HALF)])
+            if i == 3:
+                gh_grp = ring.tile([P, G, 4], BF16, name="gh_grp", tag="grp", bufs=3, align_bytes=64)
+                nc.scalar.copy(gh_grp[:], gh_raw[:].rearrange("p j w -> p w j"))
+                nc.vector.quantize_mx(out=gh_codes[:].bitcast(E4M3), scales=gh_scales[:], in_=gh_grp[:].rearrange("p w j -> p (w j)"))
+            if i >= 2:
+                out0_step(i - 2)
+            pacc(i, 1)
+            back(i, 0)
+
+        i = NU - 1
+        pacc(i, 2)
+        back(i, 1)
+        back(i, 2)
+        dzt_step(6)
+        x1_step(6, [("S", 0, 1024), ("V", 1024, LH)])
+        q_step(i)
+        m_step(i)
+        dz_quant(6)
+        xq = [out1_quant(0, 0)]
+        e_step(i)
+        dz_step(i, [("V", 0, 320), ("G", 320, HALF)])
+        out0_step(6)
+        out1_mm(0, 0, xq[0][0], xq[0][1], ["df", "df"], ["S", "S"])
+        for n in (1, 2):
+            xc, xs = out1_quant(0, n)
+            out1_mm(0, n, xc, xs, ["df", "df"], ["S", "S"])
+        dzt_step(7)
+        x1_step(7, [("S", 0, 512), ("V", 512, LH)])
+        dz_quant(7)
+        out0_step(7)
+        for n in range(3):
+            xc, xs = out1_quant(1, n)
+            out1_mm(1, n, xc, xs, ["df", "dp"], ["S", "V"])

@@ -21,9 +21,50 @@ HALF = 512
 LH = HALF * K3
 NU = 8
 
-FLOPS = 2 * B * POS * C * C + 2 * 2 * B * L * G
-BYTES = 2 * (4 * B * POS * C + B * G + G * L + C * C) + 4 * (K3 * B * C + B * G + G * L)
-
+PAR = {"warm":6,"nv":[1,1,1,1,1,1,1,1],"ps":{"tp":2,"df":2,"dp":3,"o0":1},"dummy":[0,0,0,0],"addu":[7],"half":[7],"eng":{}}
+ORDER = (
+    "warm woT00 woC00 woT01 woT03 woC01 woT02 woC02 woC03 woQ00 gT00 gC00 "
+    "woQ01 gT01 gC01 gQ0 df0.0 P00.0 dfc.0 df1.0 woT10 woC10 woT13 woC13 "
+    "woT11 woC11 P10.0 gT10 P02.0 gT11 gC10 gC11 gQ1 P11.0 woT12 woC12 "
+    "woQ10 df2.0 gT20 gT21 P22.0 P21.0 df3.0 waT0 P20.0 P01.0 P12.0 woQ11 "
+    "df0.1 P32.0 waT1 P31.0 gC20 gC21 gQ2 waC0 dfc.1 waQ0 waC1 P02.1 "
+    "pa1.0 pc1.0 P30.0 df1.1 pa0.0 P01.1 P12.1 P10.1 P00.1 P11.1 waQ1 pa2.0 "
+    "bk1.0 q10.0 pc0.0 bk0.0 df2.1 P20.1 pc2.0 gT30 P22.1 gT31 gC31 q00.0 "
+    "ma0.0 bk2.0 df3.1 q20.0 gC30 mb0.0 P21.1 P30.1 waT2 waC2 waT3 P31.1 "
+    "P32.1 df0.2 waC3 pa1.1 pc1.1 gQ3 waQ3 e10.0 e00.0 e20.0 dz0.0 df1.2 "
+    "dz1.0 dfc.2 P12.2 pa0.1 P01.2 pa2.1 bk1.1 P00.2 P11.2 pc0.1 bk0.1 waQ2 "
+    "pc2.1 df2.2 bk2.1 P10.2 q10.1 q00.1 P20.2 waT4 waC4 q20.1 P22.2 waT5 "
+    "waC5 P21.2 df3.2 P30.2 zt0.0 zt1.0 P32.2 P31.2 df0.3 gT40 gT41 waQ4 "
+    "zc1.0 zq1.0 zc0.0 gC40 zq0.0 waQ5 df1.3 P02.2 pa1.2 dfc.3 ma0.1 mb0.1 "
+    "e00.1 gC41 e20.1 e10.1 P01.3 dz0.1 dz1.1 pc1.2 ghC gQ4 P02.3 P00.3 "
+    "o0.0 pa0.2 P10.3 bk1.2 pc0.2 q10.2 pa2.2 pc2.2 P12.3 bk0.2 P11.3 q00.2 "
+    "df2.3 P22.3 P21.3 P20.3 zt0.1 zc0.1 zt1.1 bk2.2 q20.2 df3.3 P31.3 P32.3 "
+    "zc1.1 ghQ ma0.2 mb0.2 gT50 gC50 gT51 df0.4 dfc.4 zq0.1 P02.4 zq1.1 "
+    "gC51 pa1.3 df1.4 P30.3 e00.2 pc1.3 pa0.3 e10.2 pc0.3 pa2.3 e20.2 P01.4 "
+    "P12.4 bk1.3 pc2.3 dz0.2 dz1.2 o0.1 P11.4 gQ5 P10.4 q10.3 P00.4 bk2.3 "
+    "x0.2 q20.3 bk0.3 q00.3 x1.2 ma0.3 mb0.3 zt0.2 df2.4 zc0.2 zt1.2 P21.4 "
+    "P22.4 oc.1 P20.4 df3.4 P31.4 zq0.2 zc1.2 zq1.2 gT60 gT61 x2.2 df0.5 "
+    "gC60 e10.3 o0.2 pa1.4 gC61 P30.4 e20.3 e00.3 dz0.3 pc1.4 pa0.4 dz1.3 "
+    "dfc.5 pc0.4 P32.4 P01.5 bk1.4 df1.5 x0.3 P00.5 gQ6 P10.5 P11.5 pa2.4 "
+    "P12.5 bk0.4 q10.4 q00.4 ma0.4 pc2.4 zt0.3 zc0.3 df2.5 P20.5 x2.3 bk2.4 "
+    "q20.4 zt1.3 zc1.3 gT70 gC70 df3.5 gT71 P21.5 P22.5 gC71 P32.5 P31.5 "
+    "P02.5 mb0.4 P30.5 df0.6 dfc.6 P02.6 gQ7 pa2.5 x1.3 e10.4 pa1.5 e00.4 "
+    "zq0.3 e20.4 P01.6 P00.6 zq1.3 df1.6 pc2.5 bk2.5 P10.6 dz0.4 pc1.5 bk1.5 "
+    "dz1.4 pa0.5 q10.5 pc0.5 o0.3 P11.6 bk0.5 q20.5 P12.6 q00.5 df2.6 P21.6 "
+    "zt0.4 zt1.4 P22.6 df3.6 zc0.4 P20.6 ma0.5 df0.7 zc1.4 dfc.7 P32.6 P31.6 "
+    "mb0.5 pa2.6 P01.7 zq0.4 P30.6 e20.5 P02.7 e00.5 pc2.6 e10.5 dz0.5 dz1.5 "
+    "P00.7 df1.7 P12.7 pa1.6 P10.7 pa0.6 pc1.6 a12.7 P11.7 bk1.6 bk2.6 a10.7 "
+    "a11.7 q10.6 oc.3 q20.6 pc0.6 zq1.4 zt0.5 bk0.6 q00.6 ma0.6 zt1.5 df2.7 "
+    "zc1.5 df3.7 P21.7 a21.7 mb0.6 P32.7 P31.7 P22.7 P20.7 P30.7 e10.6 a22.7 "
+    "zc0.5 e00.6 o0.4 e20.6 zq0.5 zq1.5 a20.7 a30.7 dz0.6 o0.5 x0.6 oq00 "
+    "om001 q02.7 dz1.6 a31.7 q00.7 x1.6 a32.7 q10.7 om000 oc.5 q12.7 od001 "
+    "od000 zt0.6 x2.6 q20.7 oq01 om010 ma0.7 ma2.7 zc0.6 mb0.7 q22.7 om011 "
+    "od011 e00.7 od010 oq02 om021 mb2.7 zq0.6 e10.7 e20.7 od021 e12.7 e02.7 "
+    "dz0.7 zt1.6 zc1.6 zq1.6 om020 e22.7 od020 o0.6 x0.7 dz1.7 zt0.7 zt1.7 "
+    "zc0.7 zt2.7 x1.7 oq10 om101 om100 zc1.7 zc2.7 oq11 od100 om110 od101 "
+    "om111 x2.7 zq1.7 od110 zq2.7 zq0.7 od111 oq12 o0.7 oc.7 om120 om121 "
+    "od120 od121 "
+).split()
 
 def tile_hiremodule_pc_v_kernel(
     tc, h_mix, w_mix, c_proj, gate_hid, wa2, ba2, wo, bo, gate, grad_out, out_0, out_1
@@ -64,56 +105,67 @@ def tile_hiremodule_pc_v_kernel(
             for c in (0, 2):
                 nc.sync.dma_start(out=wo_nat[h][:, c : c + 2, :], in_=v[:, c : c + 2, :])
 
-        def load_g(t):
-            g_nat[t] = nat_tile("g_nat%d" % t)
-            for c in (0, 2):
-                nc.sync.dma_start(out=g_nat[t][:, c : c + 2, :], in_=g_view[:, t, c : c + 2, :])
+        def load_g(t, pairs=(0, 1)):
+            if 0 in pairs:
+                g_nat[t] = nat_tile("g_nat%d" % t)
+            for c in pairs:
+                nc.sync.dma_start(out=g_nat[t][:, 2 * c : 2 * c + 2, :], in_=g_view[:, t, 2 * c : 2 * c + 2, :])
 
         def load_wa2(w):
             wa2_nat[w] = ring.tile([P, 2, LH], BF16, name="wa2_nat%d" % w, tag="nat", bufs=3)
             v = wa2.rearrange("(m p) l -> p m l", p=P)
             nc.sync.dma_start(out=wa2_nat[w][:], in_=v[:, :, w * LH : (w + 1) * LH])
 
-        def load_st(t, pp):
+        def load_st(t, pp, fine=False):
             for k in range(K3):
                 st[t, k, pp] = ring.tile([P, 2, C], BF16, name="st%d%d%d" % (t, k, pp), tag="st", bufs=10)
-                nc.sync.dma_start(out=st[t, k, pp][:], in_=streams[k][:, t, 2 * pp : 2 * pp + 2, :])
+            for lo, hi in ((0, 1), (1, 2)) if fine else ((0, 2),):
+                for k in range(K3):
+                    nc.sync.dma_start(out=st[t, k, pp][:, lo:hi, :], in_=streams[k][:, t, 2 * pp + lo : 2 * pp + hi, :])
 
         def load_gate(t, h):
             gate_t[t, h] = ring.tile([P, K3, HALF], F32, name="gate%d%d" % (t, h), tag="gate", bufs=3)
             nc.sync.dma_start(out=gate_t[t, h][:], in_=gate_view[:, :, t, h * HALF : (h + 1) * HALF])
 
+        gh_raw = keep.tile([P, 4, G], BF16, name="gh_raw")
         load_wo(0)
-        load_g(0)
-        load_st(0, 0)
-        load_st(0, 1)
+        load_g(0, (0,))
+        load_st(0, 0, True)
+        load_g(0, (1,))
         load_wo(1)
+        load_st(0, 1)
         load_gate(0, 0)
         load_g(1)
         load_wa2(0)
-        load_gate(0, 1)
-        load_wa2(1)
         load_st(1, 0)
+        load_gate(0, 1)
         load_st(1, 1)
-        load_gate(1, 0)
+        load_wa2(1)
         load_g(2)
+        load_gate(1, 0)
         load_gate(1, 1)
-        gh_raw = keep.tile([P, 4, G], BF16, name="gh_raw")
-        nc.sync.dma_start(out=gh_raw[:], in_=gate_hid.rearrange("(p j) w -> p j w", j=4))
         load_st(2, 0)
+        nc.sync.dma_start(out=gh_raw[:], in_=gate_hid.rearrange("(p j) w -> p j w", j=4))
         load_st(2, 1)
-        load_gate(2, 0)
         load_g(3)
+        load_gate(2, 0)
         load_gate(2, 1)
         load_st(3, 0)
         load_st(3, 1)
         load_gate(3, 0)
         load_gate(3, 1)
 
-        PS_BUFS = {"tp": 2, "df": 2, "dp": 3, "o0": 1}
+        PS = PAR["ps"]
+        tasks = {}
+
+        def task(name, engine, fn):
+            tasks[name] = (engine, fn)
+
+        def eng_of(name, default):
+            return PAR["eng"].get(name, default)
 
         def bank(tag, name):
-            return psum.tile([P, HALF], F32, name=name, tag=tag, bufs=PS_BUFS[tag])
+            return psum.tile([P, HALF], F32, name=name, tag=tag, bufs=PS[tag])
 
         def copy_out(engine, out, in_):
             if engine == "S":
@@ -128,294 +180,360 @@ def tile_hiremodule_pc_v_kernel(
         def grp_tile(width, name):
             return ring.tile([P, width], BF16, name=name, tag="grp", bufs=3, align_bytes=64)
 
-        def wo_prep(h, tags, engines):
-            grp = [grp_tile(4 * HALF, "wo_grp%d%d" % (h, g)) for g in range(2)]
+        VG = {"V": nc.vector, "G": nc.gpsimd}
+        T = {}
+
+        def mk_wo(h, c):
+            tag = ("tp", "df")[c % 2] if h == 0 else "tp"
             words = wo_nat[h][:].bitcast(F32)
-            for c in range(4):
-                bk = bank(tags[c % len(tags)], "wo_ps%d%d" % (h, c))
-                word_transposes(bk, [words[:, c, 256 * g + u : 256 * (g + 1) : 2] for g in range(2) for u in range(2)])
+
+            def t():
+                T["wops", h, c] = bank(tag, "wo_ps%d%d" % (h, c))
+                word_transposes(T["wops", h, c], [words[:, c, 256 * g + u : 256 * (g + 1) : 2] for g in range(2) for u in range(2)])
+
+            e = eng_of("woC%d%d" % (h, c), "SV"[c % 2] if h == 0 else "S")
+
+            def cp():
                 for g in range(2):
-                    dst = grp[g][:, 4 * P * c : 4 * P * (c + 1)].bitcast(F32).rearrange("p (r u) -> p r u", u=2)
-                    src = bk[:, 256 * g : 256 * (g + 1)].rearrange("p (u r) -> p r u", u=2)
-                    copy_out(engines[c % len(engines)], dst, src)
-            return grp
+                    if ("wog", h, g) not in T:
+                        T["wog", h, g] = grp_tile(4 * HALF, "wo_grp%d%d" % (h, g))
+                    dst = T["wog", h, g][:, 4 * P * c : 4 * P * (c + 1)].bitcast(F32).rearrange("p (r u) -> p r u", u=2)
+                    src = T["wops", h, c][:, 256 * g : 256 * (g + 1)].rearrange("p (u r) -> p r u", u=2)
+                    copy_out(e, dst, src)
 
-        def wo_quant(h, grp):
-            for g in range(2):
-                nc.vector.quantize_mx(out=wo_codes[:, h, g, :].bitcast(E4M3), scales=wo_scales[:, h, g, :], in_=grp[g][:])
+            task("woT%d%d" % (h, c), "P", t)
+            task("woC%d%d" % (h, c), e, cp)
 
-        g_codes, g_scales, g_grp = {}, {}, {}
+        def mk_woq(h, g):
+            def f():
+                nc.vector.quantize_mx(out=wo_codes[:, h, g, :].bitcast(E4M3), scales=wo_scales[:, h, g, :], in_=T["wog", h, g][:])
 
-        def g_prep(s, tags, engines):
+            task("woQ%d%d" % (h, g), "V", f)
+
+        def mk_g(s):
             t, pair = divmod(s, 2)
-            if pair == 0:
-                g_codes[t] = ring.tile([P, 8 * P], U32, name="g_codes%d" % t, tag="g_codes", bufs=2, align_bytes=64)
-                g_scales[t] = ring.tile([P, 8 * P], U8, name="g_scales%d" % t, tag="g_scales", bufs=2, align_bytes=64)
-            g_grp[s] = grp_tile(2048, "g_grp%d" % s)
             words = g_nat[t][:].bitcast(F32)
             for q in range(2):
-                bk = bank(tags[q % len(tags)], "g_ps%d%d" % (s, q))
-                word_transposes(bk, [words[:, 2 * pair + q, 256 * g + u : 256 * (g + 1) : 2] for g in range(2) for u in range(2)])
-                dst = g_grp[s][:, 1024 * q : 1024 * (q + 1)].bitcast(F32).rearrange("p (g r u) -> p g r u", g=2, u=2)
-                src = bk[:].rearrange("p (g u r) -> p g r u", g=2, u=2)
-                copy_out(engines[q % len(engines)], dst, src)
 
-        def g_quant(s):
-            t, pair = divmod(s, 2)
-            sl = slice(512 * pair, 512 * (pair + 1))
-            nc.vector.quantize_mx(out=g_codes[t][:, sl].bitcast(E5M2), scales=g_scales[t][:, sl], in_=g_grp[s][:])
+                def tr(q=q):
+                    T["gps", s, q] = bank("dp" if s < 2 else "tp", "g_ps%d%d" % (s, q))
+                    word_transposes(T["gps", s, q], [words[:, 2 * pair + q, 256 * g + u : 256 * (g + 1) : 2] for g in range(2) for u in range(2)])
 
-        def wa2_prep(n, tag, engine):
+                e = eng_of("gC%d%d" % (s, q), "SV"[q] if s < 2 else "S")
+
+                def cp(q=q, e=e):
+                    if ("gg", s) not in T:
+                        T["gg", s] = grp_tile(2048, "g_grp%d" % s)
+                    dst = T["gg", s][:, 1024 * q : 1024 * (q + 1)].bitcast(F32).rearrange("p (g r u) -> p g r u", g=2, u=2)
+                    src = T["gps", s, q][:].rearrange("p (g u r) -> p g r u", g=2, u=2)
+                    copy_out(e, dst, src)
+
+                task("gT%d%d" % (s, q), "P", tr)
+                task("gC%d%d" % (s, q), e, cp)
+
+            def qz():
+                if ("gc", t) not in T:
+                    T["gc", t] = ring.tile([P, 8 * P], U32, name="g_codes%d" % t, tag="g_codes", bufs=2, align_bytes=64)
+                    T["gs", t] = ring.tile([P, 8 * P], U8, name="g_scales%d" % t, tag="g_scales", bufs=2, align_bytes=64)
+                sl = slice(512 * pair, 512 * (pair + 1))
+                nc.vector.quantize_mx(out=T["gc", t][:, sl].bitcast(E5M2), scales=T["gs", t][:, sl], in_=T["gg", s][:])
+
+            task("gQ%d" % s, "V", qz)
+
+        def mk_wa(n):
             w, j = divmod(n, 3)
             words = wa2_nat[w][:].bitcast(F32)
-            bk = bank(tag, "wa2_ps%d" % n)
-            word_transposes(bk, [words[:, m, 256 * j + u : 256 * (j + 1) : 2] for m in range(2) for u in range(2)])
-            grp = grp_tile(1024, "wa2_grp%d" % n)
-            dst = grp[:].bitcast(F32).rearrange("p (m r u) -> p m r u", m=2, u=2)
-            src = bk[:].rearrange("p (m u r) -> p m r u", m=2, u=2)
-            copy_out(engine, dst, src)
-            return grp
 
-        def wa2_quant(n, grp):
-            sl = slice(G * n, G * (n + 1))
-            nc.vector.quantize_mx(out=wa2_codes[:, sl].bitcast(E4M3), scales=wa2_scales[:, sl], in_=grp[:])
+            def tr():
+                T["wps", n] = bank("tp", "wa2_ps%d" % n)
+                word_transposes(T["wps", n], [words[:, m, 256 * j + u : 256 * (j + 1) : 2] for m in range(2) for u in range(2)])
 
-        df_bank, dfc, prod, dp_bank, dpt, qe, mm, z, dzg, dzc, dzs, o0_bank = {}, {}, {}, {}, {}, {}, {}, {}, {}, {}, {}, {}
+            def cp():
+                T["wg", n] = grp_tile(1024, "wa2_grp%d" % n)
+                dst = T["wg", n][:].bitcast(F32).rearrange("p (m r u) -> p m r u", m=2, u=2)
+                copy_out("S", dst, T["wps", n][:].rearrange("p (m u r) -> p m r u", m=2, u=2))
+
+            def qz():
+                sl = slice(G * n, G * (n + 1))
+                nc.vector.quantize_mx(out=wa2_codes[:, sl].bitcast(E4M3), scales=wa2_scales[:, sl], in_=T["wg", n][:])
+
+            task("waT%d" % n, "P", tr)
+            task("waC%d" % n, "S", cp)
+            task("waQ%d" % n, "V", qz)
+
+        def gh_c():
+            T["ghg"] = ring.tile([P, G, 4], BF16, name="gh_grp", tag="grp", bufs=3, align_bytes=64)
+            nc.scalar.copy(T["ghg"][:], gh_raw[:].rearrange("p j w -> p w j"))
+
+        def gh_q():
+            nc.vector.quantize_mx(out=gh_codes[:].bitcast(E4M3), scales=gh_scales[:], in_=T["ghg"][:].rearrange("p w j -> p (w j)"))
+
+        task("ghC", "S", gh_c)
+        task("ghQ", "V", gh_q)
+
         o0_sb = keep.tile([P, NT, G], F32, name="o0_sb")
 
-        def df(i, pos):
-            if i >= NU:
-                return
+        def mk_unit(i):
             t, h = divmod(i, 2)
-            bk = bank("df", "df%d%d" % (i, pos))
-            df_bank[i, pos] = bk
-            for g in range(2):
-                sl = slice(P * (2 * pos + g), P * (2 * pos + g + 1))
-                nc.tensor.matmul_mx(
-                    out=bk[:],
-                    lhsT=g_codes[t][:, sl].bitcast(E5M2),
-                    lhsT_scale=g_scales[t][:, sl],
-                    rhs=wo_codes[:, h, g, :].bitcast(E4M3),
-                    rhs_scale=wo_scales[:, h, g, :],
-                    start=(g == 0),
-                    stop=(g == 1),
-                )
+            add = i in PAR["addu"]
+            parts = ((0, 2), (2, 4)) if i in PAR["half"] else ((0, 4),)
+            nv = PAR["nv"][i]
+            def dfcf():
+                T["dfc", i] = ring.tile([P, HALF], F32, name="dfc%d" % i, tag="dfc", bufs=2)
+                nc.scalar.copy(T["dfc", i][:], T["df", i, 0][:])
 
-        def df_copy(i, pos):
-            if i >= NU:
-                return
-            dfc[i] = ring.tile([P, HALF], F32, name="dfc%d" % i, tag="dfc", bufs=2)
-            nc.scalar.copy(dfc[i][:], df_bank[i, pos][:])
+            for pos in range(POS):
 
-        def products(i, pos, engine):
-            t, h = divmod(i, 2)
+                def dff(pos=pos):
+                    bk = bank("df", "df%d%d" % (i, pos))
+                    T["df", i, pos] = bk
+                    for g, st_, sp_ in [(0, True, True)] * PAR["dummy"][pos] + [(0, True, False), (1, False, True)]:
+                        sl = slice(P * (2 * pos + g), P * (2 * pos + g + 1))
+                        nc.tensor.matmul_mx(
+                            out=bk[:],
+                            lhsT=T["gc", t][:, sl].bitcast(E5M2),
+                            lhsT_scale=T["gs", t][:, sl],
+                            rhs=wo_codes[:, h, g, :].bitcast(E4M3),
+                            rhs_scale=wo_scales[:, h, g, :],
+                            start=st_,
+                            stop=sp_,
+                        )
+
+                task("df%d.%d" % (pos, i), "P", dff)
+                if pos == 0 and nv < 3:
+                    task("dfc.%d" % i, "S", dfcf)
+                for k in range(K3):
+                    e = "G" if pos == 0 and k >= nv else "V"
+
+                    def pf(pos=pos, k=k, e=e):
+                        pt = ring.tile([P, HALF], F32, name="prod%d%d%d" % (i, pos, k), tag="prod", bufs=16)
+                        T["prod", i, pos, k] = pt
+                        s_ap = st[t, k, pos // 2][:, pos % 2, h * HALF : (h + 1) * HALF]
+                        src = T["dfc", i] if e == "G" else T["df", i, pos]
+                        VG[e].tensor_tensor(out=pt[:], in0=src[:], in1=s_ap, op=MULT)
+
+                    task("P%d%d.%d" % (pos, k, i), e, pf)
+
             for k in range(K3):
-                pt = ring.tile([P, HALF], F32, name="prod%d%d%d" % (i, pos, k), tag="prod", bufs=16)
-                prod[i, pos, k] = pt
-                s_ap = st[t, k, pos // 2][:, pos % 2, h * HALF : (h + 1) * HALF]
-                if engine == "G":
-                    nc.gpsimd.tensor_tensor(out=pt[:], in0=dfc[i][:], in1=s_ap, op=MULT)
+                if add:
+                    for pos in (1, 2, 3):
+                        e = eng_of("a%d%d.%d" % (pos, k, i), "G" if pos < 3 else "V")
+
+                        def af(pos=pos, k=k, e=e):
+                            p0 = T["prod", i, 0, k]
+                            VG[e].tensor_tensor(out=p0[:], in0=p0[:], in1=T["prod", i, pos, k][:], op=ADD)
+                            T["adn", i, k, pos] = 1
+                            if pos == 3:
+                                assert ("adn", i, k, 1) in T and ("adn", i, k, 2) in T
+                                for lo, hi in parts:
+                                    T["dp", i, k, lo] = p0[:, P * lo : P * hi]
+
+                        task("a%d%d.%d" % (pos, k, i), e, af)
                 else:
-                    nc.vector.tensor_tensor(out=pt[:], in0=df_bank[i, pos][:], in1=s_ap, op=MULT)
 
-        def pacc(i, k):
-            bk = bank("tp", "pacc%d%d" % (i, k))
-            for c in range(4):
-                cs = slice(P * c, P * (c + 1))
-                for pos in range(POS):
-                    nc.tensor.matmul(
-                        bk[:, cs], prod[i, pos, k][:, cs], ident[:], start=(pos == 0), stop=(pos == POS - 1), is_transpose=True
+                    def pacc(k=k):
+                        bk = bank("tp", "pacc%d%d" % (i, k))
+                        T["pb", i, k] = bk
+                        for c in range(4):
+                            cs = slice(P * c, P * (c + 1))
+                            for pos in range(POS):
+                                nc.tensor.matmul(
+                                    bk[:, cs], T["prod", i, pos, k][:, cs], ident[:], start=(pos == 0), stop=(pos == POS - 1), is_transpose=True
+                                )
+
+                    def pcopy(k=k):
+                        T["dpt", i, k] = ring.tile([P, HALF], F32, name="dpt%d%d" % (i, k), tag="dpt", bufs=2)
+                        nc.scalar.copy(T["dpt", i, k][:], T["pb", i, k][:])
+
+                    def back(k=k):
+                        bk = bank("dp", "dp%d%d" % (i, k))
+                        word_transposes(bk, [T["dpt", i, k][:, P * c : P * (c + 1)] for c in range(4)])
+                        for lo, hi in parts:
+                            T["dp", i, k, lo] = bk[:, P * lo : P * hi]
+
+                    task("pa%d.%d" % (k, i), "P", pacc)
+                    task("pc%d.%d" % (k, i), "S", pcopy)
+                    task("bk%d.%d" % (k, i), "P", back)
+            for lo, hi in parts:
+                cs = slice(P * lo, P * hi)
+                sfx = "%d.%d" % (lo, i)
+                late = []
+                for k in range(K3):
+
+                    def qf(k=k, lo=lo, cs=cs):
+                        if ("qe", i) not in T:
+                            T["qe", i] = ring.tile([P, K3, HALF], F32, name="qe%d" % i, tag="qe", bufs=2)
+                        nc.vector.tensor_tensor(out=T["qe", i][:, k, cs], in0=T["dp", i, k, lo][:], in1=gate_t[t, h][:, k, cs], op=MULT)
+
+                    def ef(k=k, lo=lo, cs=cs):
+                        T["ed", i, lo, k] = 1
+                        nc.vector.tensor_tensor(out=T["qe", i][:, k, cs], in0=T["dp", i, k, lo][:], in1=T["m", i, lo][:, cs], op=SUB)
+
+                    task("q%d%s" % (k, sfx), "V", qf)
+                    late.append(("e%d%s" % (k, sfx), "V", ef))
+                e = eng_of("m" + sfx, "G" if not add else "V")
+
+                def ma(lo=lo, cs=cs, e=e):
+                    T["m0", i, lo] = ring.tile([P, HALF], F32, name="m0_%d%d" % (i, lo), tag="m", bufs=2)
+                    VG[e].tensor_tensor(out=T["m0", i, lo][:, cs], in0=T["qe", i][:, 0, cs], in1=T["qe", i][:, 1, cs], op=ADD)
+
+                def mb(lo=lo, cs=cs, e=e):
+                    assert ("ed", i, lo, 0) not in T
+                    T["m", i, lo] = T["m0", i, lo]
+                    VG[e].tensor_tensor(out=T["m", i, lo][:, cs], in0=T["m0", i, lo][:, cs], in1=T["qe", i][:, 2, cs], op=ADD)
+
+                task("ma" + sfx, e, ma)
+                task("mb" + sfx, e, mb)
+                for x in late:
+                    task(*x)
+            for d in range(2):
+                e = eng_of("dz%d.%d" % (d, i), "G" if not add else "V")
+
+                def dzf(d=d, e=e):
+                    lo, hi = 256 * d, 256 * (d + 1)
+                    for l0, h0 in parts:
+                        if P * l0 < hi and lo < P * h0:
+                            assert all(("ed", i, l0, k) in T for k in range(K3))
+                    if (t // 2, h) not in z:
+                        z[t // 2, h] = ring.tile([P, 2, LH], BF16, name="z%d%d" % (t, h), tag="z", bufs=2)
+                    o = z[t // 2, h][:, t % 2, K3 * lo : K3 * hi].rearrange("p (c k) -> p c k", k=K3)
+                    a = gate_t[t, h][:, :, lo:hi].rearrange("p k c -> p c k")
+                    b = T["qe", i][:, :, lo:hi].rearrange("p k c -> p c k")
+                    VG[e].tensor_tensor(out=o, in0=a, in1=b, op=MULT)
+                    T["dzd", i, d] = 1
+
+                task("dz%d.%d" % (d, i), e, dzf)
+            if t % 2 == 1:
+                for c in range(3):
+                    e = eng_of("x%d.%d" % (c, i), "S")
+
+                    def xf(c=c, e=e):
+                        u = t // 2
+                        sl = slice(512 * c, 512 * (c + 1))
+                        copy_out(e, x1[h][:, sl, 2 * u : 2 * u + 2], z[u, h][:, :, sl].rearrange("p t l -> p l t"))
+
+                    task("x%d.%d" % (c, i), e, xf)
+            for n, (j0, j1) in enumerate(((0, 1), (1, 2), (2, 3)) if add else ((0, 2), (2, 3))):
+
+                def zt(j0=j0, j1=j1):
+                    T["zb", i, j0] = bank("tp", "dzt%d%d" % (i, j0))
+                    words = z[t // 2, h][:].bitcast(F32)
+                    word_transposes(T["zb", i, j0], [words[:, t % 2, 256 * j + u : 256 * (j + 1) : 2] for j in range(j0, j1) for u in range(2)])
+
+                def zc(j0=j0, j1=j1):
+                    nj = j1 - j0
+                    if ("dzg", i) not in T:
+                        T["dzg", i] = ring.tile([P, K3 * 512], BF16, name="dzg%d" % i, tag="dzg", bufs=2, align_bytes=64)
+                    dst = T["dzg", i][:, 512 * j0 : 512 * j1].bitcast(F32).rearrange("p (j r u) -> p j r u", j=nj, u=2)
+                    nc.scalar.copy(dst, T["zb", i, j0][:, 0 : 256 * nj].rearrange("p (j u r) -> p j r u", j=nj, u=2))
+
+                def zq(j0=j0, j1=j1):
+                    if ("dzc", i) not in T:
+                        T["dzc", i] = ring.tile([P, K3 * P], U32, name="dzc%d" % i, tag="dzc", bufs=2, align_bytes=64)
+                        T["dzs", i] = ring.tile([P, K3 * P], U8, name="dzs%d" % i, tag="dzs", bufs=2, align_bytes=64)
+                    sl = slice(P * j0, P * j1)
+                    nc.vector.quantize_mx(out=T["dzc", i][:, sl].bitcast(E5M2), scales=T["dzs", i][:, sl], in_=T["dzg", i][:, 512 * j0 : 512 * j1])
+
+                task("zt%d.%d" % (n, i), "P", zt)
+                task("zc%d.%d" % (n, i), "S", zc)
+                task("zq%d.%d" % (n, i), "V", zq)
+
+            def o0():
+                if h == 0:
+                    T["o0", t] = bank("o0", "o0_%d" % t)
+                else:
+                    assert ("o0f", t) in T
+                T["o0f", t] = 1
+                for j in range(K3):
+                    n = K3 * h + j
+                    nc.tensor.matmul_mx(
+                        out=T["o0", t][:],
+                        lhsT=T["dzc", i][:, P * j : P * (j + 1)].bitcast(E5M2),
+                        lhsT_scale=T["dzs", i][:, P * j : P * (j + 1)],
+                        rhs=wa2_codes[:, G * n : G * n + 512].bitcast(E4M3),
+                        rhs_scale=wa2_scales[:, G * n : G * n + 512],
+                        start=(n == 0),
+                        stop=(n == 5),
                     )
-            dpt[i, k] = ring.tile([P, HALF], F32, name="dpt%d%d" % (i, k), tag="dpt", bufs=2)
-            nc.scalar.copy(dpt[i, k][:], bk[:])
 
-        def back(i, k):
-            bk = bank("dp", "dp%d%d" % (i, k))
-            dp_bank[i, k] = bk
-            word_transposes(bk, [dpt[i, k][:, P * c : P * (c + 1)] for c in range(4)])
-
-        def q_step(i):
-            t, h = divmod(i, 2)
-            qe[i] = ring.tile([P, K3, HALF], F32, name="qe%d" % i, tag="qe", bufs=2)
-            for k in range(K3):
-                nc.vector.tensor_tensor(out=qe[i][:, k, :], in0=dp_bank[i, k][:], in1=gate_t[t, h][:, k, :], op=MULT)
-
-        def m_step(i):
-            m0 = ring.tile([P, HALF], F32, name="m0_%d" % i, tag="m", bufs=2)
-            nc.gpsimd.tensor_tensor(out=m0[:], in0=qe[i][:, 0, :], in1=qe[i][:, 1, :], op=ADD)
-            m1 = ring.tile([P, HALF], F32, name="m1_%d" % i, tag="m", bufs=2)
-            mm[i] = m1
-            nc.gpsimd.tensor_tensor(out=m1[:], in0=m0[:], in1=qe[i][:, 2, :], op=ADD)
-
-        def e_step(i):
-            for k in range(K3):
-                nc.vector.tensor_tensor(out=qe[i][:, k, :], in0=dp_bank[i, k][:], in1=mm[i][:], op=SUB)
-
-        def dz_step(i, parts):
-            t, h = divmod(i, 2)
-            if t % 2 == 0:
-                z[t // 2, h] = ring.tile([P, 2, LH], BF16, name="z%d%d" % (t, h), tag="z", bufs=2)
-            zt = z[t // 2, h]
-            for engine, lo, hi in parts:
-                o = zt[:, t % 2, K3 * lo : K3 * hi].rearrange("p (c k) -> p c k", k=K3)
-                a = gate_t[t, h][:, :, lo:hi].rearrange("p k c -> p c k")
-                b = qe[i][:, :, lo:hi].rearrange("p k c -> p c k")
-                eng = nc.gpsimd if engine == "G" else nc.vector
-                eng.tensor_tensor(out=o, in0=a, in1=b, op=MULT)
-
-        def x1_step(i, parts):
-            t, h = divmod(i, 2)
-            if t % 2 == 0:
-                return
-            u = t // 2
-            for engine, lo, hi in parts:
-                copy_out(engine, x1[h][:, lo:hi, 2 * u : 2 * u + 2], z[u, h][:, :, lo:hi].rearrange("p t l -> p l t"))
-
-        def dzt_step(i):
-            t, h = divmod(i, 2)
-            words = z[t // 2, h][:].bitcast(F32)
-            dzg[i] = ring.tile([P, K3 * 512], BF16, name="dzg%d" % i, tag="dzg", bufs=2, align_bytes=64)
-            for j0, nj in ((0, 2), (2, 1)):
-                bk = bank("tp", "dzt%d%d" % (i, j0))
-                word_transposes(
-                    bk,
-                    [words[:, t % 2, 256 * j + u : 256 * (j + 1) : 2] for j in range(j0, j0 + nj) for u in range(2)],
-                )
-                dst = dzg[i][:, 512 * j0 : 512 * (j0 + nj)].bitcast(F32).rearrange("p (j r u) -> p j r u", j=nj, u=2)
-                src = bk[:, 0 : 256 * nj].rearrange("p (j u r) -> p j r u", j=nj, u=2)
-                nc.scalar.copy(dst, src)
-
-        def dz_quant(i):
-            dzc[i] = ring.tile([P, K3 * P], U32, name="dzc%d" % i, tag="dzc", bufs=2, align_bytes=64)
-            dzs[i] = ring.tile([P, K3 * P], U8, name="dzs%d" % i, tag="dzs", bufs=2, align_bytes=64)
-            for lo, hi in ((0, 2), (2, 3)):
-                sl = slice(P * lo, P * hi)
-                nc.vector.quantize_mx(out=dzc[i][:, sl].bitcast(E5M2), scales=dzs[i][:, sl], in_=dzg[i][:, 512 * lo : 512 * hi])
-
-        def out0_step(i):
-            t, h = divmod(i, 2)
-            if h == 0:
-                o0_bank[t] = bank("o0", "o0_%d" % t)
-            for j in range(K3):
-                n = K3 * h + j
-                nc.tensor.matmul_mx(
-                    out=o0_bank[t][:],
-                    lhsT=dzc[i][:, P * j : P * (j + 1)].bitcast(E5M2),
-                    lhsT_scale=dzs[i][:, P * j : P * (j + 1)],
-                    rhs=wa2_codes[:, G * n : G * n + 512].bitcast(E4M3),
-                    rhs_scale=wa2_scales[:, G * n : G * n + 512],
-                    start=(n == 0),
-                    stop=(n == 5),
-                )
+            task("o0.%d" % i, "P", o0)
             if h == 1:
-                nc.scalar.copy(o0_sb[:, t, :], o0_bank[t][:, 0:G])
-                nc.sync.dma_start(out=out0_view[:, t, :], in_=o0_sb[:, t, :])
 
-        def out1_quant(h, n):
-            xc = ring.tile([P, 512], U32, name="xc%d%d" % (h, n), tag="xc", bufs=2, align_bytes=64)
-            xs = ring.tile([P, 512], U8, name="xs%d%d" % (h, n), tag="xs", bufs=2, align_bytes=64)
-            nc.vector.quantize_mx(
-                out=xc[:].bitcast(E5M2),
-                scales=xs[:],
-                in_=x1[h][:, 512 * n : 512 * (n + 1), :].rearrange("p l t -> p (l t)"),
-            )
-            return xc, xs
+                def o0c():
+                    nc.scalar.copy(o0_sb[:, t, :], T["o0", t][:, 0:G])
+                    nc.sync.dma_start(out=out0_view[:, t, :], in_=o0_sb[:, t, :])
 
-        def out1_mm(h, n, xc, xs, tags, engines):
-            for m in range(2):
-                bk = bank(tags[m], "o1_%d%d%d" % (h, n, m))
-                nc.tensor.matmul_mx(
-                    out=bk[:],
-                    lhsT=gh_codes[:, P * m : P * (m + 1)].bitcast(E4M3),
-                    lhsT_scale=gh_scales[:, P * m : P * (m + 1)],
-                    rhs=xc[:].bitcast(E5M2),
-                    rhs_scale=xs[:],
-                    start=True,
-                    stop=True,
+                task("oc.%d" % i, "S", o0c)
+
+        def mk_o1(h, n):
+            def qz():
+                T["xc", h, n] = ring.tile([P, 512], U32, name="xc%d%d" % (h, n), tag="xc", bufs=2, align_bytes=64)
+                T["xs", h, n] = ring.tile([P, 512], U8, name="xs%d%d" % (h, n), tag="xs", bufs=2, align_bytes=64)
+                nc.vector.quantize_mx(
+                    out=T["xc", h, n][:].bitcast(E5M2),
+                    scales=T["xs", h, n][:],
+                    in_=x1[h][:, 512 * n : 512 * (n + 1), :].rearrange("p l t -> p (l t)"),
                 )
-                ot = ring.tile([P, 512], F32, name="ot%d%d%d" % (h, n, m), tag="prod", bufs=16)
-                copy_out(engines[m], ot[:], bk[:])
-                l0 = LH * h + 512 * n
-                nc.sync.dma_start(out=out_1[P * m : P * (m + 1), l0 : l0 + 512], in_=ot[:])
 
-        grp0 = wo_prep(0, ["tp", "dp", "df"], ["S", "V"])
-        wo_quant(0, grp0)
-        g_prep(0, ["tp", "dp"], ["S", "V"])
-        g_quant(0)
-        g_prep(1, ["tp", "dp"], ["S", "V"])
-        df(0, 0)
-        df_copy(0, 0)
-        df(0, 1)
-        g_quant(1)
-        df(0, 2)
-        grp1 = wo_prep(1, ["tp", "dp"], ["S"])
+            task("oq%d%d" % (h, n), "V", qz)
+            for m in range(2):
 
+                def mm(m=m):
+                    T["ob", h, n, m] = bank("df", "o1_%d%d%d" % (h, n, m))
+                    nc.tensor.matmul_mx(
+                        out=T["ob", h, n, m][:],
+                        lhsT=gh_codes[:, P * m : P * (m + 1)].bitcast(E4M3),
+                        lhsT_scale=gh_scales[:, P * m : P * (m + 1)],
+                        rhs=T["xc", h, n][:].bitcast(E5M2),
+                        rhs_scale=T["xs", h, n][:],
+                        start=True,
+                        stop=True,
+                    )
+
+                e = eng_of("od%d%d%d" % (h, n, m), "S" if h == 0 or m == 0 else "V")
+
+                def cp(m=m, e=e):
+                    ot = ring.tile([P, 512], F32, name="ot%d%d%d" % (h, n, m), tag="prod", bufs=16)
+                    copy_out(e, ot[:], T["ob", h, n, m][:])
+                    l0 = LH * h + 512 * n
+                    nc.sync.dma_start(out=out_1[P * m : P * (m + 1), l0 : l0 + 512], in_=ot[:])
+
+                task("om%d%d%d" % (h, n, m), "P", mm)
+                task("od%d%d%d" % (h, n, m), e, cp)
+
+        z = {}
+        warm = keep.tile([P, HALF], BF16, name="warm")
+
+        def warm_f():
+            nc.vector.memset(warm[:], 0.0)
+            wb = bank("o0", "warm_ps")
+            for n in range(PAR["warm"]):
+                nc.tensor.matmul(wb[:], warm[:, 0:P], warm[:], start=True, stop=True)
+
+        task("warm", "P", warm_f)
+        for c in range(4):
+            mk_wo(0, c)
+        mk_g(0)
+        for g in range(2):
+            mk_woq(0, g)
+        mk_g(1)
+        for c in range(4):
+            mk_wo(1, c)
+        for g in range(2):
+            mk_woq(1, g)
+        for s in range(2, 8):
+            mk_g(s)
+        for n in range(6):
+            mk_wa(n)
         for i in range(NU):
-            products(i, 0, "G")
-            if i > 0:
-                pacc(i - 1, 2)
-                back(i - 1, 1)
-                back(i - 1, 2)
-            products(i, 1, "V")
-            df(i, 3)
-            if i + 2 < NU:
-                g_prep(i + 2, ["tp"], ["S"])
-            if i == 0:
-                wo_quant(1, grp1)
-            products(i, 2, "V")
-            df(i + 1, 0)
-            df_copy(i + 1, 0)
-            if i >= 2:
-                dzt_step(i - 2)
-                dz_quant(i - 2)
-            if i + 2 < NU:
-                g_quant(i + 2)
-            if i < 3:
-                grp = [wa2_prep(2 * i + n, "tp", "S") for n in range(2)]
-                for n in range(2):
-                    wa2_quant(2 * i + n, grp[n])
-            if i >= 1:
-                q_step(i - 1)
-                m_step(i - 1)
-            df(i + 1, 1)
-            if i >= 2:
-                x1_step(i - 2, [("S", 0, LH)])
-            products(i, 3, "V")
-            pacc(i, 0)
-            df(i + 1, 2)
-            if i >= 1:
-                e_step(i - 1)
-                dz_step(i - 1, [("G", 0, HALF)])
-            if i == 3:
-                gh_grp = ring.tile([P, G, 4], BF16, name="gh_grp", tag="grp", bufs=3, align_bytes=64)
-                nc.scalar.copy(gh_grp[:], gh_raw[:].rearrange("p j w -> p w j"))
-                nc.vector.quantize_mx(out=gh_codes[:].bitcast(E4M3), scales=gh_scales[:], in_=gh_grp[:].rearrange("p w j -> p (w j)"))
-            if i >= 2:
-                out0_step(i - 2)
-            pacc(i, 1)
-            back(i, 0)
+            mk_unit(i)
+        for h in range(2):
+            for n in range(3):
+                mk_o1(h, n)
+        DRIVER(tc, tasks, ORDER)
 
-        i = NU - 1
-        pacc(i, 2)
-        back(i, 1)
-        back(i, 2)
-        dzt_step(6)
-        x1_step(6, [("S", 0, 1024), ("V", 1024, LH)])
-        q_step(i)
-        m_step(i)
-        dz_quant(6)
-        xq = [out1_quant(0, 0)]
-        e_step(i)
-        dz_step(i, [("V", 0, 320), ("G", 320, HALF)])
-        out0_step(6)
-        out1_mm(0, 0, xq[0][0], xq[0][1], ["df", "df"], ["S", "S"])
-        for n in (1, 2):
-            xc, xs = out1_quant(0, n)
-            out1_mm(0, n, xc, xs, ["df", "df"], ["S", "S"])
-        dzt_step(7)
-        x1_step(7, [("S", 0, 512), ("V", 512, LH)])
-        dz_quant(7)
-        out0_step(7)
-        for n in range(3):
-            xc, xs = out1_quant(1, n)
-            out1_mm(1, n, xc, xs, ["df", "dp"], ["S", "V"])
+
+def DRIVER(tc, tasks, order):
+    for name in order:
+        tasks[name][1]()
+    assert set(order) == set(tasks) and len(order) == len(tasks)

from contextlib import ExitStack

import concourse.mybir as mybir
from concourse.masks import make_identity

F32 = mybir.dt.float32
BF16 = mybir.dt.bfloat16
U32 = mybir.dt.uint32
U8 = mybir.dt.uint8
E4M3 = mybir.dt.float8_e4m3fn_x4
E5M2 = mybir.dt.float8_e5m2_x4
MULT = mybir.AluOpType.mult
ADD = mybir.AluOpType.add
SUB = mybir.AluOpType.subtract

B, POS, C, G, K3 = 512, 4, 1024, 256, 3
L = C * K3
P = 128
NT = 4
HALF = 512
LH = HALF * K3
NU = 8

PAR = {"warm":6,"nv":[1,1,1,1,1,1,1,1],"ps":{"tp":2,"df":2,"dp":3,"o0":1},"dummy":[0,0,0,0],"addu":[7],"half":[7],"eng":{}}
ORDER = (
    "warm woT00 woC00 woT01 woT03 woC01 woT02 woC02 woC03 woQ00 gT00 gC00 "
    "woQ01 gT01 gC01 gQ0 df0.0 P00.0 dfc.0 df1.0 woT10 woC10 woT13 woC13 "
    "woT11 woC11 P10.0 gT10 P02.0 gT11 gC10 gC11 gQ1 P11.0 woT12 woC12 "
    "woQ10 df2.0 gT20 gT21 P22.0 P21.0 df3.0 waT0 P20.0 P01.0 P12.0 woQ11 "
    "df0.1 P32.0 waT1 P31.0 gC20 gC21 gQ2 waC0 dfc.1 waQ0 waC1 P02.1 "
    "pa1.0 pc1.0 P30.0 df1.1 pa0.0 P01.1 P12.1 P10.1 P00.1 P11.1 waQ1 pa2.0 "
    "bk1.0 q10.0 pc0.0 bk0.0 df2.1 P20.1 pc2.0 gT30 P22.1 gT31 gC31 q00.0 "
    "ma0.0 bk2.0 df3.1 q20.0 gC30 mb0.0 P21.1 P30.1 waT2 waC2 waT3 P31.1 "
    "P32.1 df0.2 waC3 pa1.1 pc1.1 gQ3 waQ3 e10.0 e00.0 e20.0 dz0.0 df1.2 "
    "dz1.0 dfc.2 P12.2 pa0.1 P01.2 pa2.1 bk1.1 P00.2 P11.2 pc0.1 bk0.1 waQ2 "
    "pc2.1 df2.2 bk2.1 P10.2 q10.1 q00.1 P20.2 waT4 waC4 q20.1 P22.2 waT5 "
    "waC5 P21.2 df3.2 P30.2 zt0.0 zt1.0 P32.2 P31.2 df0.3 gT40 gT41 waQ4 "
    "zc1.0 zq1.0 zc0.0 gC40 zq0.0 waQ5 df1.3 P02.2 pa1.2 dfc.3 ma0.1 mb0.1 "
    "e00.1 gC41 e20.1 e10.1 P01.3 dz0.1 dz1.1 pc1.2 ghC gQ4 P02.3 P00.3 "
    "o0.0 pa0.2 P10.3 bk1.2 pc0.2 q10.2 pa2.2 pc2.2 P12.3 bk0.2 P11.3 q00.2 "
    "df2.3 P22.3 P21.3 P20.3 zt0.1 zc0.1 zt1.1 bk2.2 q20.2 df3.3 P31.3 P32.3 "
    "zc1.1 ghQ ma0.2 mb0.2 gT50 gC50 gT51 df0.4 dfc.4 zq0.1 P02.4 zq1.1 "
    "gC51 pa1.3 df1.4 P30.3 e00.2 pc1.3 pa0.3 e10.2 pc0.3 pa2.3 e20.2 P01.4 "
    "P12.4 bk1.3 pc2.3 dz0.2 dz1.2 o0.1 P11.4 gQ5 P10.4 q10.3 P00.4 bk2.3 "
    "x0.2 q20.3 bk0.3 q00.3 x1.2 ma0.3 mb0.3 zt0.2 df2.4 zc0.2 zt1.2 P21.4 "
    "P22.4 oc.1 P20.4 df3.4 P31.4 zq0.2 zc1.2 zq1.2 gT60 gT61 x2.2 df0.5 "
    "gC60 e10.3 o0.2 pa1.4 gC61 P30.4 e20.3 e00.3 dz0.3 pc1.4 pa0.4 dz1.3 "
    "dfc.5 pc0.4 P32.4 P01.5 bk1.4 df1.5 x0.3 P00.5 gQ6 P10.5 P11.5 pa2.4 "
    "P12.5 bk0.4 q10.4 q00.4 ma0.4 pc2.4 zt0.3 zc0.3 df2.5 P20.5 x2.3 bk2.4 "
    "q20.4 zt1.3 zc1.3 gT70 gC70 df3.5 gT71 P21.5 P22.5 gC71 P32.5 P31.5 "
    "P02.5 mb0.4 P30.5 df0.6 dfc.6 P02.6 gQ7 pa2.5 x1.3 e10.4 pa1.5 e00.4 "
    "zq0.3 e20.4 P01.6 P00.6 zq1.3 df1.6 pc2.5 bk2.5 P10.6 dz0.4 pc1.5 bk1.5 "
    "dz1.4 pa0.5 q10.5 pc0.5 o0.3 P11.6 bk0.5 q20.5 P12.6 q00.5 df2.6 P21.6 "
    "zt0.4 zt1.4 P22.6 df3.6 zc0.4 P20.6 ma0.5 df0.7 zc1.4 dfc.7 P32.6 P31.6 "
    "mb0.5 pa2.6 P01.7 zq0.4 P30.6 e20.5 P02.7 e00.5 pc2.6 e10.5 dz0.5 dz1.5 "
    "P00.7 df1.7 P12.7 pa1.6 P10.7 pa0.6 pc1.6 a12.7 P11.7 bk1.6 bk2.6 a10.7 "
    "a11.7 q10.6 oc.3 q20.6 pc0.6 zq1.4 zt0.5 bk0.6 q00.6 ma0.6 zt1.5 df2.7 "
    "zc1.5 df3.7 P21.7 a21.7 mb0.6 P32.7 P31.7 P22.7 P20.7 P30.7 e10.6 a22.7 "
    "zc0.5 e00.6 o0.4 e20.6 zq0.5 zq1.5 a20.7 a30.7 dz0.6 o0.5 x0.6 oq00 "
    "om001 q02.7 dz1.6 a31.7 q00.7 x1.6 a32.7 q10.7 om000 oc.5 q12.7 od001 "
    "od000 zt0.6 x2.6 q20.7 oq01 om010 ma0.7 ma2.7 zc0.6 mb0.7 q22.7 om011 "
    "od011 e00.7 od010 oq02 om021 mb2.7 zq0.6 e10.7 e20.7 od021 e12.7 e02.7 "
    "dz0.7 zt1.6 zc1.6 zq1.6 om020 e22.7 od020 o0.6 x0.7 dz1.7 zt0.7 zt1.7 "
    "zc0.7 zt2.7 x1.7 oq10 om101 om100 zc1.7 zc2.7 oq11 od100 om110 od101 "
    "om111 x2.7 zq1.7 od110 zq2.7 zq0.7 od111 oq12 o0.7 oc.7 om120 om121 "
    "od120 od121 "
).split()

def tile_hiremodule_pc_v_kernel(
    tc, h_mix, w_mix, c_proj, gate_hid, wa2, ba2, wo, bo, gate, grad_out, out_0, out_1
):
    nc = tc.nc
    with ExitStack() as ctx:
        keep = ctx.enter_context(tc.tile_pool(name="keep", bufs=1))
        ring = ctx.enter_context(tc.tile_pool(name="ring", bufs=2))
        psum = ctx.enter_context(tc.psum_pool(name="psum", bufs=2))
        ctx.enter_context(tc.manual_schedule())

        streams = [x.rearrange("(p t) i j c -> p t (i j) c", t=NT) for x in (h_mix, w_mix, c_proj)]
        g_view = grad_out.rearrange("(p t) i j c -> p t (i j) c", t=NT)
        gate_view = gate.rearrange("k (p t) c -> p k t c", t=NT)
        out0_view = out_0.rearrange("(p t) g -> p t g", t=NT)

        ident = keep.tile([P, P], F32, name="ident")
        make_identity(nc, ident[:])

        wo_codes = keep.tile([P, 2, 2, HALF], U32, name="wo_codes", align_bytes=64)
        wo_scales = keep.tile([P, 2, 2, HALF], U8, name="wo_scales", align_bytes=64)
        wa2_codes = keep.tile([P, 7 * G], U32, name="wa2_codes", align_bytes=64)
        wa2_scales = keep.tile([P, 7 * G], U8, name="wa2_scales", align_bytes=64)
        gh_codes = keep.tile([P, G], U32, name="gh_codes", align_bytes=64)
        gh_scales = keep.tile([P, G], U8, name="gh_scales", align_bytes=64)
        x1 = [keep.tile([P, LH, 4], BF16, name="x1_%d" % h, align_bytes=64) for h in range(2)]
        nc.gpsimd.memset(wa2_codes[:, 6 * G : 7 * G], 0)
        nc.gpsimd.memset(wa2_scales[:, 6 * G : 7 * G], 0)

        def nat_tile(name):
            return ring.tile([P, 4, C], BF16, name=name, tag="nat", bufs=3)

        wo_nat, g_nat, wa2_nat, st, gate_t = {}, {}, {}, {}, {}

        def load_wo(h):
            wo_nat[h] = nat_tile("wo_nat%d" % h)
            v = wo[h * HALF : (h + 1) * HALF, :].rearrange("(c p) o -> p c o", p=P)
            for c in (0, 2):
                nc.sync.dma_start(out=wo_nat[h][:, c : c + 2, :], in_=v[:, c : c + 2, :])

        def load_g(t, pairs=(0, 1)):
            if 0 in pairs:
                g_nat[t] = nat_tile("g_nat%d" % t)
            for c in pairs:
                nc.sync.dma_start(out=g_nat[t][:, 2 * c : 2 * c + 2, :], in_=g_view[:, t, 2 * c : 2 * c + 2, :])

        def load_wa2(w):
            wa2_nat[w] = ring.tile([P, 2, LH], BF16, name="wa2_nat%d" % w, tag="nat", bufs=3)
            v = wa2.rearrange("(m p) l -> p m l", p=P)
            nc.sync.dma_start(out=wa2_nat[w][:], in_=v[:, :, w * LH : (w + 1) * LH])

        def load_st(t, pp, fine=False):
            for k in range(K3):
                st[t, k, pp] = ring.tile([P, 2, C], BF16, name="st%d%d%d" % (t, k, pp), tag="st", bufs=10)
            for lo, hi in ((0, 1), (1, 2)) if fine else ((0, 2),):
                for k in range(K3):
                    nc.sync.dma_start(out=st[t, k, pp][:, lo:hi, :], in_=streams[k][:, t, 2 * pp + lo : 2 * pp + hi, :])

        def load_gate(t, h):
            gate_t[t, h] = ring.tile([P, K3, HALF], F32, name="gate%d%d" % (t, h), tag="gate", bufs=3)
            nc.sync.dma_start(out=gate_t[t, h][:], in_=gate_view[:, :, t, h * HALF : (h + 1) * HALF])

        gh_raw = keep.tile([P, 4, G], BF16, name="gh_raw")
        load_wo(0)
        load_g(0, (0,))
        load_st(0, 0, True)
        load_g(0, (1,))
        load_wo(1)
        load_st(0, 1)
        load_gate(0, 0)
        load_g(1)
        load_wa2(0)
        load_st(1, 0)
        load_gate(0, 1)
        load_st(1, 1)
        load_wa2(1)
        load_g(2)
        load_gate(1, 0)
        load_gate(1, 1)
        load_st(2, 0)
        nc.sync.dma_start(out=gh_raw[:], in_=gate_hid.rearrange("(p j) w -> p j w", j=4))
        load_st(2, 1)
        load_g(3)
        load_gate(2, 0)
        load_gate(2, 1)
        load_st(3, 0)
        load_st(3, 1)
        load_gate(3, 0)
        load_gate(3, 1)

        PS = PAR["ps"]
        tasks = {}

        def task(name, engine, fn):
            tasks[name] = (engine, fn)

        def eng_of(name, default):
            return PAR["eng"].get(name, default)

        def bank(tag, name):
            return psum.tile([P, HALF], F32, name=name, tag=tag, bufs=PS[tag])

        def copy_out(engine, out, in_):
            if engine == "S":
                nc.scalar.copy(out, in_)
            else:
                nc.vector.tensor_copy(out, in_)

        def word_transposes(bk, srcs):
            for n, src in enumerate(srcs):
                nc.tensor.transpose(bk[:, n * P : (n + 1) * P], src, ident[:])

        def grp_tile(width, name):
            return ring.tile([P, width], BF16, name=name, tag="grp", bufs=3, align_bytes=64)

        VG = {"V": nc.vector, "G": nc.gpsimd}
        T = {}

        def mk_wo(h, c):
            tag = ("tp", "df")[c % 2] if h == 0 else "tp"
            words = wo_nat[h][:].bitcast(F32)

            def t():
                T["wops", h, c] = bank(tag, "wo_ps%d%d" % (h, c))
                word_transposes(T["wops", h, c], [words[:, c, 256 * g + u : 256 * (g + 1) : 2] for g in range(2) for u in range(2)])

            e = eng_of("woC%d%d" % (h, c), "SV"[c % 2] if h == 0 else "S")

            def cp():
                for g in range(2):
                    if ("wog", h, g) not in T:
                        T["wog", h, g] = grp_tile(4 * HALF, "wo_grp%d%d" % (h, g))
                    dst = T["wog", h, g][:, 4 * P * c : 4 * P * (c + 1)].bitcast(F32).rearrange("p (r u) -> p r u", u=2)
                    src = T["wops", h, c][:, 256 * g : 256 * (g + 1)].rearrange("p (u r) -> p r u", u=2)
                    copy_out(e, dst, src)

            task("woT%d%d" % (h, c), "P", t)
            task("woC%d%d" % (h, c), e, cp)

        def mk_woq(h, g):
            def f():
                nc.vector.quantize_mx(out=wo_codes[:, h, g, :].bitcast(E4M3), scales=wo_scales[:, h, g, :], in_=T["wog", h, g][:])

            task("woQ%d%d" % (h, g), "V", f)

        def mk_g(s):
            t, pair = divmod(s, 2)
            words = g_nat[t][:].bitcast(F32)
            for q in range(2):

                def tr(q=q):
                    T["gps", s, q] = bank("dp" if s < 2 else "tp", "g_ps%d%d" % (s, q))
                    word_transposes(T["gps", s, q], [words[:, 2 * pair + q, 256 * g + u : 256 * (g + 1) : 2] for g in range(2) for u in range(2)])

                e = eng_of("gC%d%d" % (s, q), "SV"[q] if s < 2 else "S")

                def cp(q=q, e=e):
                    if ("gg", s) not in T:
                        T["gg", s] = grp_tile(2048, "g_grp%d" % s)
                    dst = T["gg", s][:, 1024 * q : 1024 * (q + 1)].bitcast(F32).rearrange("p (g r u) -> p g r u", g=2, u=2)
                    src = T["gps", s, q][:].rearrange("p (g u r) -> p g r u", g=2, u=2)
                    copy_out(e, dst, src)

                task("gT%d%d" % (s, q), "P", tr)
                task("gC%d%d" % (s, q), e, cp)

            def qz():
                if ("gc", t) not in T:
                    T["gc", t] = ring.tile([P, 8 * P], U32, name="g_codes%d" % t, tag="g_codes", bufs=2, align_bytes=64)
                    T["gs", t] = ring.tile([P, 8 * P], U8, name="g_scales%d" % t, tag="g_scales", bufs=2, align_bytes=64)
                sl = slice(512 * pair, 512 * (pair + 1))
                nc.vector.quantize_mx(out=T["gc", t][:, sl].bitcast(E5M2), scales=T["gs", t][:, sl], in_=T["gg", s][:])

            task("gQ%d" % s, "V", qz)

        def mk_wa(n):
            w, j = divmod(n, 3)
            words = wa2_nat[w][:].bitcast(F32)

            def tr():
                T["wps", n] = bank("tp", "wa2_ps%d" % n)
                word_transposes(T["wps", n], [words[:, m, 256 * j + u : 256 * (j + 1) : 2] for m in range(2) for u in range(2)])

            def cp():
                T["wg", n] = grp_tile(1024, "wa2_grp%d" % n)
                dst = T["wg", n][:].bitcast(F32).rearrange("p (m r u) -> p m r u", m=2, u=2)
                copy_out("S", dst, T["wps", n][:].rearrange("p (m u r) -> p m r u", m=2, u=2))

            def qz():
                sl = slice(G * n, G * (n + 1))
                nc.vector.quantize_mx(out=wa2_codes[:, sl].bitcast(E4M3), scales=wa2_scales[:, sl], in_=T["wg", n][:])

            task("waT%d" % n, "P", tr)
            task("waC%d" % n, "S", cp)
            task("waQ%d" % n, "V", qz)

        def gh_c():
            T["ghg"] = ring.tile([P, G, 4], BF16, name="gh_grp", tag="grp", bufs=3, align_bytes=64)
            nc.scalar.copy(T["ghg"][:], gh_raw[:].rearrange("p j w -> p w j"))

        def gh_q():
            nc.vector.quantize_mx(out=gh_codes[:].bitcast(E4M3), scales=gh_scales[:], in_=T["ghg"][:].rearrange("p w j -> p (w j)"))

        task("ghC", "S", gh_c)
        task("ghQ", "V", gh_q)

        o0_sb = keep.tile([P, NT, G], F32, name="o0_sb")

        def mk_unit(i):
            t, h = divmod(i, 2)
            add = i in PAR["addu"]
            parts = ((0, 2), (2, 4)) if i in PAR["half"] else ((0, 4),)
            nv = PAR["nv"][i]
            def dfcf():
                T["dfc", i] = ring.tile([P, HALF], F32, name="dfc%d" % i, tag="dfc", bufs=2)
                nc.scalar.copy(T["dfc", i][:], T["df", i, 0][:])

            for pos in range(POS):

                def dff(pos=pos):
                    bk = bank("df", "df%d%d" % (i, pos))
                    T["df", i, pos] = bk
                    for g, st_, sp_ in [(0, True, True)] * PAR["dummy"][pos] + [(0, True, False), (1, False, True)]:
                        sl = slice(P * (2 * pos + g), P * (2 * pos + g + 1))
                        nc.tensor.matmul_mx(
                            out=bk[:],
                            lhsT=T["gc", t][:, sl].bitcast(E5M2),
                            lhsT_scale=T["gs", t][:, sl],
                            rhs=wo_codes[:, h, g, :].bitcast(E4M3),
                            rhs_scale=wo_scales[:, h, g, :],
                            start=st_,
                            stop=sp_,
                        )

                task("df%d.%d" % (pos, i), "P", dff)
                if pos == 0 and nv < 3:
                    task("dfc.%d" % i, "S", dfcf)
                for k in range(K3):
                    e = "G" if pos == 0 and k >= nv else "V"

                    def pf(pos=pos, k=k, e=e):
                        pt = ring.tile([P, HALF], F32, name="prod%d%d%d" % (i, pos, k), tag="prod", bufs=16)
                        T["prod", i, pos, k] = pt
                        s_ap = st[t, k, pos // 2][:, pos % 2, h * HALF : (h + 1) * HALF]
                        src = T["dfc", i] if e == "G" else T["df", i, pos]
                        VG[e].tensor_tensor(out=pt[:], in0=src[:], in1=s_ap, op=MULT)

                    task("P%d%d.%d" % (pos, k, i), e, pf)

            for k in range(K3):
                if add:
                    for pos in (1, 2, 3):
                        e = eng_of("a%d%d.%d" % (pos, k, i), "G" if pos < 3 else "V")

                        def af(pos=pos, k=k, e=e):
                            p0 = T["prod", i, 0, k]
                            VG[e].tensor_tensor(out=p0[:], in0=p0[:], in1=T["prod", i, pos, k][:], op=ADD)
                            T["adn", i, k, pos] = 1
                            if pos == 3:
                                assert ("adn", i, k, 1) in T and ("adn", i, k, 2) in T
                                for lo, hi in parts:
                                    T["dp", i, k, lo] = p0[:, P * lo : P * hi]

                        task("a%d%d.%d" % (pos, k, i), e, af)
                else:

                    def pacc(k=k):
                        bk = bank("tp", "pacc%d%d" % (i, k))
                        T["pb", i, k] = bk
                        for c in range(4):
                            cs = slice(P * c, P * (c + 1))
                            for pos in range(POS):
                                nc.tensor.matmul(
                                    bk[:, cs], T["prod", i, pos, k][:, cs], ident[:], start=(pos == 0), stop=(pos == POS - 1), is_transpose=True
                                )

                    def pcopy(k=k):
                        T["dpt", i, k] = ring.tile([P, HALF], F32, name="dpt%d%d" % (i, k), tag="dpt", bufs=2)
                        nc.scalar.copy(T["dpt", i, k][:], T["pb", i, k][:])

                    def back(k=k):
                        bk = bank("dp", "dp%d%d" % (i, k))
                        word_transposes(bk, [T["dpt", i, k][:, P * c : P * (c + 1)] for c in range(4)])
                        for lo, hi in parts:
                            T["dp", i, k, lo] = bk[:, P * lo : P * hi]

                    task("pa%d.%d" % (k, i), "P", pacc)
                    task("pc%d.%d" % (k, i), "S", pcopy)
                    task("bk%d.%d" % (k, i), "P", back)
            for lo, hi in parts:
                cs = slice(P * lo, P * hi)
                sfx = "%d.%d" % (lo, i)
                late = []
                for k in range(K3):

                    def qf(k=k, lo=lo, cs=cs):
                        if ("qe", i) not in T:
                            T["qe", i] = ring.tile([P, K3, HALF], F32, name="qe%d" % i, tag="qe", bufs=2)
                        nc.vector.tensor_tensor(out=T["qe", i][:, k, cs], in0=T["dp", i, k, lo][:], in1=gate_t[t, h][:, k, cs], op=MULT)

                    def ef(k=k, lo=lo, cs=cs):
                        T["ed", i, lo, k] = 1
                        nc.vector.tensor_tensor(out=T["qe", i][:, k, cs], in0=T["dp", i, k, lo][:], in1=T["m", i, lo][:, cs], op=SUB)

                    task("q%d%s" % (k, sfx), "V", qf)
                    late.append(("e%d%s" % (k, sfx), "V", ef))
                e = eng_of("m" + sfx, "G" if not add else "V")

                def ma(lo=lo, cs=cs, e=e):
                    T["m0", i, lo] = ring.tile([P, HALF], F32, name="m0_%d%d" % (i, lo), tag="m", bufs=2)
                    VG[e].tensor_tensor(out=T["m0", i, lo][:, cs], in0=T["qe", i][:, 0, cs], in1=T["qe", i][:, 1, cs], op=ADD)

                def mb(lo=lo, cs=cs, e=e):
                    assert ("ed", i, lo, 0) not in T
                    T["m", i, lo] = T["m0", i, lo]
                    VG[e].tensor_tensor(out=T["m", i, lo][:, cs], in0=T["m0", i, lo][:, cs], in1=T["qe", i][:, 2, cs], op=ADD)

                task("ma" + sfx, e, ma)
                task("mb" + sfx, e, mb)
                for x in late:
                    task(*x)
            for d in range(2):
                e = eng_of("dz%d.%d" % (d, i), "G" if not add else "V")

                def dzf(d=d, e=e):
                    lo, hi = 256 * d, 256 * (d + 1)
                    for l0, h0 in parts:
                        if P * l0 < hi and lo < P * h0:
                            assert all(("ed", i, l0, k) in T for k in range(K3))
                    if (t // 2, h) not in z:
                        z[t // 2, h] = ring.tile([P, 2, LH], BF16, name="z%d%d" % (t, h), tag="z", bufs=2)
                    o = z[t // 2, h][:, t % 2, K3 * lo : K3 * hi].rearrange("p (c k) -> p c k", k=K3)
                    a = gate_t[t, h][:, :, lo:hi].rearrange("p k c -> p c k")
                    b = T["qe", i][:, :, lo:hi].rearrange("p k c -> p c k")
                    VG[e].tensor_tensor(out=o, in0=a, in1=b, op=MULT)
                    T["dzd", i, d] = 1

                task("dz%d.%d" % (d, i), e, dzf)
            if t % 2 == 1:
                for c in range(3):
                    e = eng_of("x%d.%d" % (c, i), "S")

                    def xf(c=c, e=e):
                        u = t // 2
                        sl = slice(512 * c, 512 * (c + 1))
                        copy_out(e, x1[h][:, sl, 2 * u : 2 * u + 2], z[u, h][:, :, sl].rearrange("p t l -> p l t"))

                    task("x%d.%d" % (c, i), e, xf)
            for n, (j0, j1) in enumerate(((0, 1), (1, 2), (2, 3)) if add else ((0, 2), (2, 3))):

                def zt(j0=j0, j1=j1):
                    T["zb", i, j0] = bank("tp", "dzt%d%d" % (i, j0))
                    words = z[t // 2, h][:].bitcast(F32)
                    word_transposes(T["zb", i, j0], [words[:, t % 2, 256 * j + u : 256 * (j + 1) : 2] for j in range(j0, j1) for u in range(2)])

                def zc(j0=j0, j1=j1):
                    nj = j1 - j0
                    if ("dzg", i) not in T:
                        T["dzg", i] = ring.tile([P, K3 * 512], BF16, name="dzg%d" % i, tag="dzg", bufs=2, align_bytes=64)
                    dst = T["dzg", i][:, 512 * j0 : 512 * j1].bitcast(F32).rearrange("p (j r u) -> p j r u", j=nj, u=2)
                    nc.scalar.copy(dst, T["zb", i, j0][:, 0 : 256 * nj].rearrange("p (j u r) -> p j r u", j=nj, u=2))

                def zq(j0=j0, j1=j1):
                    if ("dzc", i) not in T:
                        T["dzc", i] = ring.tile([P, K3 * P], U32, name="dzc%d" % i, tag="dzc", bufs=2, align_bytes=64)
                        T["dzs", i] = ring.tile([P, K3 * P], U8, name="dzs%d" % i, tag="dzs", bufs=2, align_bytes=64)
                    sl = slice(P * j0, P * j1)
                    nc.vector.quantize_mx(out=T["dzc", i][:, sl].bitcast(E5M2), scales=T["dzs", i][:, sl], in_=T["dzg", i][:, 512 * j0 : 512 * j1])

                task("zt%d.%d" % (n, i), "P", zt)
                task("zc%d.%d" % (n, i), "S", zc)
                task("zq%d.%d" % (n, i), "V", zq)

            def o0():
                if h == 0:
                    T["o0", t] = bank("o0", "o0_%d" % t)
                else:
                    assert ("o0f", t) in T
                T["o0f", t] = 1
                for j in range(K3):
                    n = K3 * h + j
                    nc.tensor.matmul_mx(
                        out=T["o0", t][:],
                        lhsT=T["dzc", i][:, P * j : P * (j + 1)].bitcast(E5M2),
                        lhsT_scale=T["dzs", i][:, P * j : P * (j + 1)],
                        rhs=wa2_codes[:, G * n : G * n + 512].bitcast(E4M3),
                        rhs_scale=wa2_scales[:, G * n : G * n + 512],
                        start=(n == 0),
                        stop=(n == 5),
                    )

            task("o0.%d" % i, "P", o0)
            if h == 1:

                def o0c():
                    nc.scalar.copy(o0_sb[:, t, :], T["o0", t][:, 0:G])
                    nc.sync.dma_start(out=out0_view[:, t, :], in_=o0_sb[:, t, :])

                task("oc.%d" % i, "S", o0c)

        def mk_o1(h, n):
            def qz():
                T["xc", h, n] = ring.tile([P, 512], U32, name="xc%d%d" % (h, n), tag="xc", bufs=2, align_bytes=64)
                T["xs", h, n] = ring.tile([P, 512], U8, name="xs%d%d" % (h, n), tag="xs", bufs=2, align_bytes=64)
                nc.vector.quantize_mx(
                    out=T["xc", h, n][:].bitcast(E5M2),
                    scales=T["xs", h, n][:],
                    in_=x1[h][:, 512 * n : 512 * (n + 1), :].rearrange("p l t -> p (l t)"),
                )

            task("oq%d%d" % (h, n), "V", qz)
            for m in range(2):

                def mm(m=m):
                    T["ob", h, n, m] = bank("df", "o1_%d%d%d" % (h, n, m))
                    nc.tensor.matmul_mx(
                        out=T["ob", h, n, m][:],
                        lhsT=gh_codes[:, P * m : P * (m + 1)].bitcast(E4M3),
                        lhsT_scale=gh_scales[:, P * m : P * (m + 1)],
                        rhs=T["xc", h, n][:].bitcast(E5M2),
                        rhs_scale=T["xs", h, n][:],
                        start=True,
                        stop=True,
                    )

                e = eng_of("od%d%d%d" % (h, n, m), "S" if h == 0 or m == 0 else "V")

                def cp(m=m, e=e):
                    ot = ring.tile([P, 512], F32, name="ot%d%d%d" % (h, n, m), tag="prod", bufs=16)
                    copy_out(e, ot[:], T["ob", h, n, m][:])
                    l0 = LH * h + 512 * n
                    nc.sync.dma_start(out=out_1[P * m : P * (m + 1), l0 : l0 + 512], in_=ot[:])

                task("om%d%d%d" % (h, n, m), "P", mm)
                task("od%d%d%d" % (h, n, m), e, cp)

        z = {}
        warm = keep.tile([P, HALF], BF16, name="warm")

        def warm_f():
            nc.vector.memset(warm[:], 0.0)
            wb = bank("o0", "warm_ps")
            for n in range(PAR["warm"]):
                nc.tensor.matmul(wb[:], warm[:, 0:P], warm[:], start=True, stop=True)

        task("warm", "P", warm_f)
        for c in range(4):
            mk_wo(0, c)
        mk_g(0)
        for g in range(2):
            mk_woq(0, g)
        mk_g(1)
        for c in range(4):
            mk_wo(1, c)
        for g in range(2):
            mk_woq(1, g)
        for s in range(2, 8):
            mk_g(s)
        for n in range(6):
            mk_wa(n)
        for i in range(NU):
            mk_unit(i)
        for h in range(2):
            for n in range(3):
                mk_o1(h, n)
        DRIVER(tc, tasks, ORDER)


def DRIVER(tc, tasks, order):
    for name in order:
        tasks[name][1]()
    assert set(order) == set(tasks) and len(order) == len(tasks)
